import numpy as np
import ml_dtypes


def mxq(x, axis, fmt="e4m3"):
    dtype, down = {"e4m3": (ml_dtypes.float8_e4m3fn, 7), "e5m2": (ml_dtypes.float8_e5m2, 14)}[fmt]
    v = np.moveaxis(np.asarray(x, np.float32).astype(ml_dtypes.bfloat16).astype(np.float64), axis, -1)
    blocks = v.reshape(v.shape[:-1] + (-1, 32))
    amax = np.abs(blocks).max(-1, keepdims=True)
    byte = np.maximum(np.where(amax > 0, np.frexp(amax)[1] - 1 + 127, 0) - down, 1)
    scale = np.exp2(byte - 127.0)
    codes = (blocks / scale).astype(np.float32).astype(dtype).astype(np.float64)
    return np.moveaxis((codes * scale).reshape(v.shape), -1, axis)


WIDE = False


def mx_kscale(k):
    if not WIDE:
        return np.ones(k)
    levels = np.array([10, -10, 5, -5, 0])
    a = np.random.permutation(np.resize(levels, k // 512 * 4)).reshape(k // 512, 4)
    idx = np.arange(k)
    return np.exp2(a[idx // 512, idx % 128 // 32])


BF16 = ml_dtypes.bfloat16


def bf(x):
    return np.asarray(x, np.float32).astype(BF16)


def f64(x):
    return np.asarray(x).astype(np.float64)


B, N, D, H, L, C = 16, 512, 512, 8, 3, 2
HD = D // H


def setup_inputs():
    s, t = mx_kscale(D), mx_kscale(D)
    tk = t.reshape(H, HD)[:, :L]
    return {
        "fields": bf((np.random.standard_normal((B, N, D)) + np.random.standard_normal((B, 1, D))) * t),
        "h2": bf(np.maximum(np.random.standard_normal((B, N, D)), 0.0) * 1.4 * s),
        "corr_kernels": bf(np.random.standard_normal((H, L, L)) * 2.5 / tk[:, None, :]),
        "w3": bf(np.random.standard_normal((D, D)) * 1.5 / np.sqrt(D) * t[:, None] / s[None, :]),
        "b3": bf(np.random.standard_normal(D) * 0.3 * t),
        "out_w": bf(np.random.standard_normal((D, D)) / np.sqrt(D) / t[None, :]),
        "out_b": bf(np.random.standard_normal(D) * 0.3),
        "inter_w": bf(1.0 + 0.5 * np.random.standard_normal(C)),
    }


def reference(fields, h2, corr_kernels, w3, b3, out_w, out_b, inter_w):
    f = f64(fields).reshape(B, N, H, HD)
    ck = f64(corr_kernels)
    corr = np.zeros((B, N, H, HD))
    for lag in range(1, L + 1):
        base = f[:, :-lag]
        shifted = f[:, lag:]
        w = np.pad(ck[:, lag - 1, :], ((0, 0), (0, HD - L)))
        mean_shift = shifted.mean(axis=1, keepdims=True)
        cw = base * w[None, None] * mean_shift
        corr = corr + np.pad(cw, ((0, 0), (0, lag), (0, 0), (0, 0)))
    corr = corr / L
    nl = ((mxq(f64(h2), 2, "e4m3") @ mxq(f64(w3), 1, "e4m3").T) + f64(b3)).reshape(B, N, H, HD)
    r = f64(inter_w)
    e = np.exp(r - r.max())
    iw = e / e.sum()
    enhanced = (f + iw[0] * corr + iw[1] * nl).reshape(B, N, D)
    return (mxq(enhanced, 2, "e4m3") @ mxq(f64(out_w), 1, "e4m3").T) + f64(out_b)

@@ -1,0 +1,422 @@
+from contextlib import ExitStack
+
+import concourse.mybir as mybir
+from concourse.masks import make_identity
+
+F32 = mybir.dt.float32
+BF16 = mybir.dt.bfloat16
+U32 = mybir.dt.uint32
+U8 = mybir.dt.uint8
+FP8X4 = mybir.dt.float8_e4m3fn_x4
+ALU = mybir.AluOpType
+ACT = mybir.ActivationFunctionType
+AXIS = mybir.AxisListType
+
+P = 128
+B = 16
+N = 512
+D = 512
+HEADS = 8
+HEAD_DIM = D // HEADS
+LAGS = 3
+TILES = N // P
+PLANES = 4
+HALVES = 2
+ROW = TILES * D
+KERNEL_CHANNELS = 4
+SUMS = HEADS * KERNEL_CHANNELS
+SCALES = TILES * PLANES
+HELD = 9
+WEIGHTED = (TILES - 1) * PLANES * HELD
+LOADS_AHEAD = 4
+OUT_TILES_ON_VECTOR = 2
+
+FLOPS = 2 * 2 * B * N * D * D
+
+
+def tile_fieldinteractionoperators_pa_t_kernel(
+    tc, fields, h2, corr_kernels, w3, b3, out_w, out_b, inter_w, out
+):
+    nc = tc.nc
+    with ExitStack() as ctx:
+        ctx.enter_context(tc.manual_schedule())
+        const = ctx.enter_context(tc.tile_pool(name="const", bufs=1))
+        rows_in = ctx.enter_context(tc.tile_pool(name="rows_in", bufs=LOADS_AHEAD))
+        weights_in = ctx.enter_context(tc.tile_pool(name="weights_in", bufs=2))
+        work = ctx.enter_context(tc.tile_pool(name="work", bufs=2))
+        rows_out = ctx.enter_context(tc.tile_pool(name="rows_out", bufs=3))
+        transposed = ctx.enter_context(tc.psum_pool(name="transposed", bufs=2))
+        products = ctx.enter_context(tc.psum_pool(name="products", bufs=3))
+        totals = ctx.enter_context(tc.psum_pool(name="totals", bufs=1))
+
+        identity = const.tile([P, P], F32)
+        make_identity(nc, identity[:])
+        vector_rows = const.tile([P, 768], BF16)
+        nc.vector.memset(vector_rows[:], 0.0)
+        b3_rows = const.tile([P, D // HALVES], BF16)
+        nc.vector.memset(b3_rows[:], 0.0)
+        edge_rows = const.tile([P, ROW], BF16)
+        nc.vector.memset(edge_rows[:], 0.0)
+        ones = const.tile([P, P], BF16)
+        nc.vector.memset(ones[:], 1.0)
+        zero_column = const.tile([P, 1], F32)
+        nc.vector.memset(zero_column[:], 0.0)
+        lag_weight = const.tile([P, LAGS * SUMS], F32)
+        nc.vector.memset(lag_weight[:], 0.0)
+        scales_all = const.tile([P, B * SCALES], F32)
+        nc.vector.memset(scales_all[:], 1.0)
+
+        nc.scalar.dma_start(out=vector_rows[0:1, 640:642], in_=inter_w.rearrange("(o c) -> o c", o=1))
+        nc.scalar.dma_start(
+            out=vector_rows[0:1, 512:584], in_=corr_kernels.rearrange("(o h) l j -> o (h l j)", o=1)
+        )
+        nc.scalar.dma_start(out=edge_rows[0:B, :], in_=fields[:, 0:TILES, :].rearrange("b n c -> b (n c)"))
+        nc.scalar.dma_start(
+            out=edge_rows[B : 2 * B, :], in_=fields[:, N - TILES : N, :].rearrange("b n c -> b (n c)")
+        )
+        nc.scalar.dma_start(out=b3_rows[0:HALVES, :], in_=b3.rearrange("(u c) -> u c", u=HALVES))
+        nc.scalar.dma_start(out=vector_rows[0:1, 0:D], in_=out_b.rearrange("(o c) -> o c", o=1))
+
+        w3_rows = weights_in.tile([P, ROW], BF16, tag="weight_rows")
+        nc.sync.dma_start(
+            out=w3_rows[:].rearrange("m (u x) -> m u x", u=HALVES),
+            in_=w3.rearrange("(u m e) k -> m u (e k)", u=HALVES, e=2),
+        )
+        out_w_rows = weights_in.tile([P, ROW], BF16, tag="weight_rows")
+        nc.sync.dma_start(
+            out=out_w_rows[:].rearrange("m (a k) -> m a k", a=TILES),
+            in_=out_w.rearrange("(a m) k -> m a k", a=TILES),
+        )
+
+        h_rows = {}
+        f_rows = {}
+
+        def load(b):
+            h_tile = rows_in.tile([P, ROW], BF16, tag="h_rows")
+            nc.sync.dma_start(out=h_tile[:], in_=h2[b].rearrange("(p i) c -> p (i c)", i=TILES))
+            h_rows[b] = h_tile
+            f_tile = rows_in.tile([P, ROW], BF16, tag="f_rows")
+            nc.sync.dma_start(out=f_tile[:], in_=fields[b].rearrange("(p i) c -> p (i c)", i=TILES))
+            f_rows[b] = f_tile
+
+        for b in range(LOADS_AHEAD):
+            load(b)
+
+        def rows_to_words(rows, grouped):
+            words = rows[:].bitcast(F32)
+            grouped_words = grouped[:].bitcast(F32)
+            for pair in range(TILES // 2):
+                bank = transposed.tile([P, 512], F32, tag="row_words")
+                for k in range(2):
+                    for u in range(HALVES):
+                        first = (2 * pair + k) * (D // 2) + u * P
+                        nc.tensor.transpose(
+                            bank[:, (HALVES * k + u) * P : (HALVES * k + u + 1) * P],
+                            words[:, first : first + P],
+                            identity[:],
+                        )
+                nc.scalar.copy(
+                    out=grouped_words[:, pair * 512 : (pair + 1) * 512].rearrange(
+                        "q (k r u) -> q k r u", k=2, u=HALVES
+                    ),
+                    in_=bank[:].rearrange("q (k u r) -> q k r u", k=2, u=HALVES),
+                )
+
+        def quantise(grouped, codes, scales):
+            nc.vector.quantize_mx(out=codes[:].bitcast(FP8X4), scales=scales[:], in_=grouped[:])
+
+        warm = const.tile([P, 1], F32)
+        nc.scalar.activation(out=warm[:], in_=zero_column[:], func=ACT.Exp)
+
+        spread_small_ps = products.tile([P, 512], F32, tag="product")
+        nc.tensor.matmul(
+            out=spread_small_ps[:, 0:256], lhsT=ones[:], rhs=vector_rows[:, 512:768], start=True, stop=True
+        )
+        spread_small = const.tile([P, 256], F32)
+        nc.vector.tensor_copy(out=spread_small[:], in_=spread_small_ps[:, 0:256])
+
+        logits = spread_small[:, 128:130]
+        top = const.tile([P, 1], F32)
+        nc.vector.tensor_tensor(out=top[:], in0=logits[:, 0:1], in1=logits[:, 1:2], op=ALU.max)
+        minus_top = const.tile([P, 1], F32)
+        nc.vector.tensor_scalar_mul(out=minus_top[:], in0=top[:], scalar1=-1.0)
+        exps = const.tile([P, 2], F32)
+        exp_sum = const.tile([P, 1], F32)
+        nc.scalar.activation(
+            out=exps[:], in_=logits, func=ACT.Exp, bias=minus_top[:, 0:1], scale=1.0, accum_out=exp_sum[:, 0:1]
+        )
+        inv_sum = const.tile([P, 1], F32)
+        nc.vector.reciprocal(out=inv_sum[:], in_=exp_sum[:])
+        iw = const.tile([P, 2], F32)
+        nc.vector.tensor_scalar_mul(out=iw[:], in0=exps[:], scalar1=inv_sum[:, 0:1])
+
+        b3_ps = products.tile([P, 512], F32, tag="product")
+        nc.tensor.transpose(b3_ps[:, 0:P], b3_rows[:].bitcast(F32), identity[:])
+        nl_bias = const.tile([P, PLANES], F32)
+        nc.vector.tensor_scalar_mul(out=nl_bias[:], in0=b3_ps[:, 0:HALVES].bitcast(BF16), scalar1=iw[:, 1:2])
+
+        out_bias_ps = products.tile([P, 512], F32, tag="product")
+        nc.tensor.matmul(out=out_bias_ps[:], lhsT=ones[:], rhs=vector_rows[:, 0:D], start=True, stop=True)
+        out_bias = const.tile([P, D], F32)
+        nc.vector.tensor_copy(out=out_bias[:], in_=out_bias_ps[:])
+
+        first_tokens = const.tile([P, B * SCALES], F32)
+        last_tokens = const.tile([P, B * SCALES], F32)
+        edge_words = edge_rows[:].bitcast(F32)
+        for u in range(HALVES):
+            edge_bank = transposed.tile([P, 512], F32, tag="field_words")
+            for n in range(TILES):
+                first = n * (D // 2) + u * P
+                nc.tensor.transpose(edge_bank[:, n * P : (n + 1) * P], edge_words[:, first : first + P], identity[:])
+            edge_values = edge_bank[:].bitcast(BF16).rearrange("q (n c e) -> q n c e", n=TILES, e=2)
+            for tokens, first_row in ((first_tokens, 0), (last_tokens, B)):
+                nc.vector.tensor_copy(
+                    out=tokens[:].rearrange("q (b n u e) -> q n b u e", b=B, n=TILES, e=2)[:, :, :, u, :],
+                    in_=edge_values[:, :, first_row : first_row + B, :],
+                )
+
+        w3_grouped = work.tile([P, PLANES * 512], BF16, tag="row_grouped", align_bytes=64)
+        rows_to_words(w3_rows, w3_grouped)
+        out_w_grouped = work.tile([P, PLANES * 512], BF16, tag="row_grouped", align_bytes=64)
+        rows_to_words(out_w_rows, out_w_grouped)
+
+        kernels = spread_small[:, 0:72].rearrange("p (h l j) -> p l h j", h=HEADS, l=LAGS)
+        lag_weight_hj = lag_weight[:].rearrange("p (l h j) -> p l h j", l=LAGS, h=HEADS)
+        for lag in range(1, LAGS + 1):
+            nc.vector.tensor_scalar(
+                out=lag_weight_hj[:, lag - 1, :, 0:LAGS],
+                in0=kernels[:, lag - 1],
+                scalar1=iw[:, 0:1],
+                scalar2=1.0 / (LAGS * (N - lag)),
+                op0=ALU.mult,
+                op1=ALU.mult,
+            )
+        own_weight = const.tile([P, LAGS * SUMS], F32)
+        lives_here = identity[:].rearrange("p (g x) -> p g x", x=32)[:, :, 0:2].unsqueeze(1)
+        for e in range(2):
+            nc.vector.tensor_tensor(
+                out=own_weight[:].rearrange("p (a g r e) -> p a g r e", g=4, r=2, e=2)[:, :, :, :, e],
+                in0=lag_weight[:].rearrange("p (a g r e) -> p a g r e", g=4, r=2, e=2)[:, :, :, :, e],
+                in1=lives_here.to_broadcast([P, LAGS * HALVES, 4, 2]),
+                op=ALU.mult,
+            )
+        plane_weight = const.tile([P, LAGS * PLANES], F32)
+        nc.vector.tensor_reduce(
+            out=plane_weight[:].rearrange("p (a e) -> p a e", e=2),
+            in_=own_weight[:].rearrange("p (a m e) -> p a e m", m=8, e=2),
+            axis=AXIS.X,
+            op=ALU.add,
+        )
+        total_weight = const.tile([P, (TILES - 1) * SUMS], F32)
+        for lag in range(1, LAGS + 1):
+            i = LAGS - lag
+            if lag == 1:
+                nc.vector.tensor_copy(
+                    out=total_weight[:, i * SUMS : (i + 1) * SUMS], in_=own_weight[:, 0:SUMS]
+                )
+            else:
+                nc.vector.tensor_tensor(
+                    out=total_weight[:, i * SUMS : (i + 1) * SUMS],
+                    in0=total_weight[:, (i + 1) * SUMS : (i + 2) * SUMS],
+                    in1=own_weight[:, (lag - 1) * SUMS : lag * SUMS],
+                    op=ALU.add,
+                )
+
+        weighted_all = const.tile([P, B * WEIGHTED], F32)
+        held = weighted_all[:].rearrange("q (b i u m e) -> q b i u m e", b=B, i=TILES - 1, u=HALVES, e=2)
+        scales_bite = scales_all[:].rearrange("q (b i u e) -> q b i u e", b=B, i=TILES, e=2)
+        first_bnue = first_tokens[:].rearrange("q (b n u e) -> q b n u e", b=B, n=TILES, e=2)
+        head = first_bnue[:, :, 0]
+        for lag in range(1, LAGS + 1):
+            i = LAGS - lag
+            if lag > 1:
+                longer = const.tile([P, B * PLANES], F32, name="head%d" % lag)
+                longer_bue = longer[:].rearrange("q (b u e) -> q b u e", b=B, e=2)
+                nc.vector.tensor_tensor(out=longer_bue, in0=head, in1=first_bnue[:, :, lag - 1], op=ALU.add)
+                head = longer_bue
+            head_term = const.tile([P, B * PLANES], F32, name="head_term%d" % lag)
+            head_term_bue = head_term[:].rearrange("q (b u e) -> q b u e", b=B, e=2)
+            nc.vector.tensor_tensor(
+                out=head_term_bue,
+                in0=head,
+                in1=plane_weight[:, (lag - 1) * PLANES : lag * PLANES]
+                .rearrange("q (u e) -> q u e", e=2)
+                .unsqueeze(1)
+                .to_broadcast([P, B, HALVES, 2]),
+                op=ALU.mult,
+            )
+            before = scales_bite[:, :, TILES - 1] if lag == 1 else held[:, :, i + 1, :, HELD - 1, :]
+            nc.vector.tensor_tensor(out=held[:, :, i, :, HELD - 1, :], in0=before, in1=head_term_bue, op=ALU.subtract)
+
+        w3_codes = const.tile([P, D], U32, align_bytes=64)
+        w3_scales = const.tile([P, D], U8, align_bytes=64)
+        quantise(w3_grouped, w3_codes, w3_scales)
+        out_w_codes = const.tile([P, D], U32, align_bytes=64)
+        out_w_scales = const.tile([P, D], U8, align_bytes=64)
+        quantise(out_w_grouped, out_w_codes, out_w_scales)
+
+        h_grouped = {}
+        h_codes = {}
+        h_scales = {}
+        field_banks = {}
+        field_totals = {}
+        field_terms = {}
+        enhanced = {}
+        e_codes = {}
+        e_scales = {}
+
+        def transposes(b):
+            grouped = work.tile([P, PLANES * N], BF16, tag="row_grouped", align_bytes=64)
+            rows_to_words(h_rows[b], grouped)
+            h_grouped[b] = grouped
+            f_tile = f_rows[b]
+            total = totals.tile([P, SUMS], F32, tag="total")
+            kernel_channels = f_tile[:].rearrange("p (i h x) -> p i h x", i=TILES, h=HEADS)
+            for i in range(TILES):
+                nc.tensor.matmul(
+                    out=total[:].rearrange("p (h j) -> p h j", h=HEADS),
+                    lhsT=ones[:],
+                    rhs=kernel_channels[:, i, :, 0:KERNEL_CHANNELS],
+                    start=(i == 0),
+                    stop=(i == TILES - 1),
+                )
+            field_totals[b] = total
+            f_words = f_tile[:].bitcast(F32)
+            banks = []
+            for u in range(HALVES):
+                bank = transposed.tile([P, N], F32, tag="field_words")
+                for i in range(TILES):
+                    first = i * (D // 2) + u * P
+                    nc.tensor.transpose(bank[:, i * P : (i + 1) * P], f_words[:, first : first + P], identity[:])
+                banks.append(bank)
+            field_banks[b] = banks
+
+        def field_scales_products(b):
+            nc.vector.tensor_tensor(
+                out=weighted_all[:, b * WEIGHTED : (b + 1) * WEIGHTED].rearrange(
+                    "q (i u x) -> q i u x", i=TILES - 1, u=HALVES
+                )[:, :, :, 0:16],
+                in0=field_totals[b][:]
+                .rearrange("q (u x) -> q u x", u=HALVES)
+                .unsqueeze(1)
+                .to_broadcast([P, TILES - 1, HALVES, 16]),
+                in1=total_weight[:].rearrange("q (i u x) -> q i u x", i=TILES - 1, u=HALVES),
+                op=ALU.mult,
+            )
+
+        def field_scales_sums(b):
+            nc.vector.tensor_reduce(
+                out=scales_all[:, b * SCALES : b * SCALES + (TILES - 1) * PLANES].rearrange("q (a e) -> q a e", e=2),
+                in_=weighted_all[:, b * WEIGHTED : (b + 1) * WEIGHTED].rearrange("q (a m e) -> q a e m", m=HELD, e=2),
+                axis=AXIS.X,
+                op=ALU.add,
+            )
+
+        def field_term(b):
+            term = work.tile([P, PLANES * N], F32, tag="field_term")
+            banks = field_banks[b]
+            for u in range(HALVES):
+                values = banks[u][:].bitcast(BF16).rearrange("q (x e) -> q x e", e=2)
+                for e in range(2):
+                    t = 2 * u + e
+                    nc.scalar.activation(
+                        out=term[:, t * N : (t + 1) * N],
+                        in_=values[:, :, e],
+                        func=ACT.Identity,
+                        bias=nl_bias[:, t : t + 1],
+                        scale=scales_all[:, b * SCALES + t : b * SCALES + t + 1],
+                    )
+            last_scaled = work.tile([P, SCALES], F32, tag="last_scaled")
+            nc.gpsimd.tensor_tensor(
+                out=last_scaled[:],
+                in0=last_tokens[:, b * SCALES : (b + 1) * SCALES],
+                in1=scales_all[:, b * SCALES : (b + 1) * SCALES],
+                op=ALU.mult,
+            )
+            nc.gpsimd.tensor_tensor(
+                out=term[:].rearrange("q (t i r) -> q i t r", t=PLANES, i=TILES)[:, :, :, P - 1],
+                in0=last_scaled[:].rearrange("q (i t) -> q i t", i=TILES),
+                in1=nl_bias[:].unsqueeze(1).to_broadcast([P, TILES, PLANES]),
+                op=ALU.add,
+            )
+            field_terms[b] = term
+
+        def quantise_h(b):
+            codes = work.tile([P, N], U32, tag="h_codes", align_bytes=64)
+            scales = work.tile([P, N], U8, tag="h_scales", align_bytes=64)
+            quantise(h_grouped[b], codes, scales)
+            h_codes[b] = codes
+            h_scales[b] = scales
+
+        def first_product_and_fusion(b):
+            fused = work.tile([P, PLANES * N], BF16, tag="enhanced", align_bytes=64)
+            term = field_terms[b]
+            for i in range(TILES):
+                tokens = slice(i * P, (i + 1) * P)
+                nl = products.tile([P, PLANES * P], F32, tag="product")
+                for t in range(PLANES):
+                    channels = slice(t * P, (t + 1) * P)
+                    nc.tensor.matmul_mx(
+                        out=nl[:, channels],
+                        lhsT=w3_codes[:, channels].bitcast(FP8X4),
+                        lhsT_scale=w3_scales[:, channels],
+                        rhs=h_codes[b][:, tokens].bitcast(FP8X4),
+                        rhs_scale=h_scales[b][:, tokens],
+                        start=True,
+                        stop=True,
+                    )
+                nc.vector.scalar_tensor_tensor(
+                    out=fused[:, i * PLANES * P : (i + 1) * PLANES * P].rearrange("q (r t) -> q r t", t=PLANES),
+                    in0=nl[:].rearrange("q (t r) -> q r t", t=PLANES),
+                    scalar=iw[:, 1:2],
+                    in1=term[:].rearrange("q (t i r) -> q i r t", t=PLANES, i=TILES)[:, i],
+                    op0=ALU.mult,
+                    op1=ALU.add,
+                )
+            enhanced[b] = fused
+
+        def quantise_enhanced(b):
+            codes = work.tile([P, N], U32, tag="e_codes", align_bytes=64)
+            scales = work.tile([P, N], U8, tag="e_scales", align_bytes=64)
+            quantise(enhanced[b], codes, scales)
+            e_codes[b] = codes
+            e_scales[b] = scales
+
+        def second_product_and_store(b):
+            result = rows_out.tile([P, TILES * D], F32, tag="result")
+            for i in range(TILES):
+                tokens = slice(i * P, (i + 1) * P)
+                columns = slice(i * D, (i + 1) * D)
+                projected = products.tile([P, D], F32, tag="product")
+                nc.tensor.matmul_mx(
+                    out=projected[:],
+                    lhsT=e_codes[b][:, tokens].bitcast(FP8X4),
+                    lhsT_scale=e_scales[b][:, tokens],
+                    rhs=out_w_codes[:].bitcast(FP8X4),
+                    rhs_scale=out_w_scales[:],
+                    start=True,
+                    stop=True,
+                )
+                if i < OUT_TILES_ON_VECTOR:
+                    nc.vector.tensor_tensor(out=result[:, columns], in0=projected[:], in1=out_bias[:], op=ALU.add)
+                else:
+                    nc.scalar.copy(out=result[:, columns], in_=projected[:])
+                    nc.gpsimd.tensor_tensor(out=result[:, columns], in0=result[:, columns], in1=out_bias[:], op=ALU.add)
+            nc.sync.dma_start(out=out[b].rearrange("(p i) o -> p (i o)", i=TILES), in_=result[:])
+
+        for j in range(-2, B + 1):
+            if 0 <= j and j + LOADS_AHEAD < B:
+                load(j + LOADS_AHEAD)
+            if 0 <= j + 1 < B:
+                field_scales_products(j + 1)
+                quantise_h(j + 1)
+                field_scales_sums(j + 1)
+                field_term(j + 1)
+            if 0 <= j < B:
+                first_product_and_fusion(j)
+            if 0 <= j - 1 < B:
+                second_product_and_store(j - 1)
+            if 0 <= j < B:
+                quantise_enhanced(j)
+            if 0 <= j + 2 < B:
+                transposes(j + 2)

@@ -28,8 +28,9 @@ SUMS = HEADS * KERNEL_CHANNELS
 SCALES = TILES * PLANES
 HELD = 9
 WEIGHTED = (TILES - 1) * PLANES * HELD
-LOADS_AHEAD = 4
-OUT_TILES_ON_VECTOR = 2
+LOADS_AHEAD = 5
+ROW_BUFFERS = 4
+OUT_TILES_ON_SCALAR = 2
 
 FLOPS = 2 * 2 * B * N * D * D
 
@@ -41,12 +42,13 @@ def tile_fieldinteractionoperators_pa_t_kernel(
     with ExitStack() as ctx:
         ctx.enter_context(tc.manual_schedule())
         const = ctx.enter_context(tc.tile_pool(name="const", bufs=1))
-        rows_in = ctx.enter_context(tc.tile_pool(name="rows_in", bufs=LOADS_AHEAD))
+        rows_in = ctx.enter_context(tc.tile_pool(name="rows_in", bufs=ROW_BUFFERS))
         weights_in = ctx.enter_context(tc.tile_pool(name="weights_in", bufs=2))
         work = ctx.enter_context(tc.tile_pool(name="work", bufs=2))
+        terms = ctx.enter_context(tc.tile_pool(name="terms", bufs=3))
         rows_out = ctx.enter_context(tc.tile_pool(name="rows_out", bufs=3))
-        transposed = ctx.enter_context(tc.psum_pool(name="transposed", bufs=2))
-        products = ctx.enter_context(tc.psum_pool(name="products", bufs=3))
+        transposed = ctx.enter_context(tc.psum_pool(name="transposed", bufs=3))
+        products = ctx.enter_context(tc.psum_pool(name="products", bufs=4))
         totals = ctx.enter_context(tc.psum_pool(name="totals", bufs=1))
 
         identity = const.tile([P, P], F32)
@@ -99,28 +101,22 @@ def tile_fieldinteractionoperators_pa_t_kernel(
             nc.sync.dma_start(out=f_tile[:], in_=fields[b].rearrange("(p i) c -> p (i c)", i=TILES))
             f_rows[b] = f_tile
 
-        for b in range(LOADS_AHEAD):
-            load(b)
-
-        def rows_to_words(rows, grouped):
+        def rows_to_words(rows, grouped, pair):
             words = rows[:].bitcast(F32)
             grouped_words = grouped[:].bitcast(F32)
-            for pair in range(TILES // 2):
-                bank = transposed.tile([P, 512], F32, tag="row_words")
-                for k in range(2):
-                    for u in range(HALVES):
-                        first = (2 * pair + k) * (D // 2) + u * P
-                        nc.tensor.transpose(
-                            bank[:, (HALVES * k + u) * P : (HALVES * k + u + 1) * P],
-                            words[:, first : first + P],
-                            identity[:],
-                        )
-                nc.scalar.copy(
-                    out=grouped_words[:, pair * 512 : (pair + 1) * 512].rearrange(
-                        "q (k r u) -> q k r u", k=2, u=HALVES
-                    ),
-                    in_=bank[:].rearrange("q (k u r) -> q k r u", k=2, u=HALVES),
-                )
+            bank = transposed.tile([P, 512], F32, tag="words")
+            for k in range(2):
+                for u in range(HALVES):
+                    first = (2 * pair + k) * (D // 2) + u * P
+                    nc.tensor.transpose(
+                        bank[:, (HALVES * k + u) * P : (HALVES * k + u + 1) * P],
+                        words[:, first : first + P],
+                        identity[:],
+                    )
+            nc.scalar.copy(
+                out=grouped_words[:, pair * 512 : (pair + 1) * 512].rearrange("q (k r u) -> q k r u", k=2, u=HALVES),
+                in_=bank[:].rearrange("q (k u r) -> q k r u", k=2, u=HALVES),
+            )
 
         def quantise(grouped, codes, scales):
             nc.vector.quantize_mx(out=codes[:].bitcast(FP8X4), scales=scales[:], in_=grouped[:])
@@ -164,7 +160,7 @@ def tile_fieldinteractionoperators_pa_t_kernel(
         last_tokens = const.tile([P, B * SCALES], F32)
         edge_words = edge_rows[:].bitcast(F32)
         for u in range(HALVES):
-            edge_bank = transposed.tile([P, 512], F32, tag="field_words")
+            edge_bank = transposed.tile([P, 512], F32, tag="words")
             for n in range(TILES):
                 first = n * (D // 2) + u * P
                 nc.tensor.transpose(edge_bank[:, n * P : (n + 1) * P], edge_words[:, first : first + P], identity[:])
@@ -176,9 +172,11 @@ def tile_fieldinteractionoperators_pa_t_kernel(
                 )
 
         w3_grouped = work.tile([P, PLANES * 512], BF16, tag="row_grouped", align_bytes=64)
-        rows_to_words(w3_rows, w3_grouped)
         out_w_grouped = work.tile([P, PLANES * 512], BF16, tag="row_grouped", align_bytes=64)
-        rows_to_words(out_w_rows, out_w_grouped)
+        for pair in range(TILES // 2):
+            rows_to_words(w3_rows, w3_grouped, pair)
+        for pair in range(TILES // 2):
+            rows_to_words(out_w_rows, out_w_grouped, pair)
 
         kernels = spread_small[:, 0:72].rearrange("p (h l j) -> p l h j", h=HEADS, l=LAGS)
         lag_weight_hj = lag_weight[:].rearrange("p (l h j) -> p l h j", l=LAGS, h=HEADS)
@@ -258,20 +256,16 @@ def tile_fieldinteractionoperators_pa_t_kernel(
         h_grouped = {}
         h_codes = {}
         h_scales = {}
-        field_banks = {}
         field_totals = {}
         field_terms = {}
         enhanced = {}
         e_codes = {}
         e_scales = {}
+        results = {}
 
-        def transposes(b):
-            grouped = work.tile([P, PLANES * N], BF16, tag="row_grouped", align_bytes=64)
-            rows_to_words(h_rows[b], grouped)
-            h_grouped[b] = grouped
-            f_tile = f_rows[b]
+        def total_fields(b):
             total = totals.tile([P, SUMS], F32, tag="total")
-            kernel_channels = f_tile[:].rearrange("p (i h x) -> p i h x", i=TILES, h=HEADS)
+            kernel_channels = f_rows[b][:].rearrange("p (i h x) -> p i h x", i=TILES, h=HEADS)
             for i in range(TILES):
                 nc.tensor.matmul(
                     out=total[:].rearrange("p (h j) -> p h j", h=HEADS),
@@ -281,15 +275,32 @@ def tile_fieldinteractionoperators_pa_t_kernel(
                     stop=(i == TILES - 1),
                 )
             field_totals[b] = total
-            f_words = f_tile[:].bitcast(F32)
-            banks = []
-            for u in range(HALVES):
-                bank = transposed.tile([P, N], F32, tag="field_words")
-                for i in range(TILES):
-                    first = i * (D // 2) + u * P
-                    nc.tensor.transpose(bank[:, i * P : (i + 1) * P], f_words[:, first : first + P], identity[:])
-                banks.append(bank)
-            field_banks[b] = banks
+
+        def transpose_h(b, pair):
+            if pair == 0:
+                grouped = work.tile([P, PLANES * N], BF16, tag="row_grouped", align_bytes=64)
+                h_grouped[b] = grouped
+            rows_to_words(h_rows[b], h_grouped[b], pair)
+
+        def transpose_fields(b, u):
+            if u == 0:
+                term = terms.tile([P, PLANES * N], F32, tag="field_term")
+                field_terms[b] = term
+            f_words = f_rows[b][:].bitcast(F32)
+            bank = transposed.tile([P, N], F32, tag="words")
+            for i in range(TILES):
+                first = i * (D // 2) + u * P
+                nc.tensor.transpose(bank[:, i * P : (i + 1) * P], f_words[:, first : first + P], identity[:])
+            values = bank[:].bitcast(BF16).rearrange("q (x e) -> q x e", e=2)
+            for e in range(2):
+                t = 2 * u + e
+                nc.scalar.activation(
+                    out=field_terms[b][:, t * N : (t + 1) * N],
+                    in_=values[:, :, e],
+                    func=ACT.Identity,
+                    bias=nl_bias[:, t : t + 1],
+                    scale=scales_all[:, b * SCALES + t : b * SCALES + t + 1],
+                )
 
         def field_scales_products(b):
             nc.vector.tensor_tensor(
@@ -312,20 +323,8 @@ def tile_fieldinteractionoperators_pa_t_kernel(
                 op=ALU.add,
             )
 
-        def field_term(b):
-            term = work.tile([P, PLANES * N], F32, tag="field_term")
-            banks = field_banks[b]
-            for u in range(HALVES):
-                values = banks[u][:].bitcast(BF16).rearrange("q (x e) -> q x e", e=2)
-                for e in range(2):
-                    t = 2 * u + e
-                    nc.scalar.activation(
-                        out=term[:, t * N : (t + 1) * N],
-                        in_=values[:, :, e],
-                        func=ACT.Identity,
-                        bias=nl_bias[:, t : t + 1],
-                        scale=scales_all[:, b * SCALES + t : b * SCALES + t + 1],
-                    )
+        def last_rows(b):
+            term = field_terms[b]
             last_scaled = work.tile([P, SCALES], F32, tag="last_scaled")
             nc.gpsimd.tensor_tensor(
                 out=last_scaled[:],
@@ -339,7 +338,6 @@ def tile_fieldinteractionoperators_pa_t_kernel(
                 in1=nl_bias[:].unsqueeze(1).to_broadcast([P, TILES, PLANES]),
                 op=ALU.add,
             )
-            field_terms[b] = term
 
         def quantise_h(b):
             codes = work.tile([P, N], U32, tag="h_codes", align_bytes=64)
@@ -348,32 +346,31 @@ def tile_fieldinteractionoperators_pa_t_kernel(
             h_codes[b] = codes
             h_scales[b] = scales
 
-        def first_product_and_fusion(b):
-            fused = work.tile([P, PLANES * N], BF16, tag="enhanced", align_bytes=64)
-            term = field_terms[b]
-            for i in range(TILES):
-                tokens = slice(i * P, (i + 1) * P)
-                nl = products.tile([P, PLANES * P], F32, tag="product")
-                for t in range(PLANES):
-                    channels = slice(t * P, (t + 1) * P)
-                    nc.tensor.matmul_mx(
-                        out=nl[:, channels],
-                        lhsT=w3_codes[:, channels].bitcast(FP8X4),
-                        lhsT_scale=w3_scales[:, channels],
-                        rhs=h_codes[b][:, tokens].bitcast(FP8X4),
-                        rhs_scale=h_scales[b][:, tokens],
-                        start=True,
-                        stop=True,
-                    )
-                nc.vector.scalar_tensor_tensor(
-                    out=fused[:, i * PLANES * P : (i + 1) * PLANES * P].rearrange("q (r t) -> q r t", t=PLANES),
-                    in0=nl[:].rearrange("q (t r) -> q r t", t=PLANES),
-                    scalar=iw[:, 1:2],
-                    in1=term[:].rearrange("q (t i r) -> q i r t", t=PLANES, i=TILES)[:, i],
-                    op0=ALU.mult,
-                    op1=ALU.add,
+        def first_product_and_fusion(b, i):
+            if i == 0:
+                fused = work.tile([P, PLANES * N], BF16, tag="enhanced", align_bytes=64)
+                enhanced[b] = fused
+            tokens = slice(i * P, (i + 1) * P)
+            nl = products.tile([P, PLANES * P], F32, tag="product")
+            for t in range(PLANES):
+                channels = slice(t * P, (t + 1) * P)
+                nc.tensor.matmul_mx(
+                    out=nl[:, channels],
+                    lhsT=w3_codes[:, channels].bitcast(FP8X4),
+                    lhsT_scale=w3_scales[:, channels],
+                    rhs=h_codes[b][:, tokens].bitcast(FP8X4),
+                    rhs_scale=h_scales[b][:, tokens],
+                    start=True,
+                    stop=True,
                 )
-            enhanced[b] = fused
+            nc.vector.scalar_tensor_tensor(
+                out=enhanced[b][:, i * PLANES * P : (i + 1) * PLANES * P].rearrange("q (r t) -> q r t", t=PLANES),
+                in0=nl[:].rearrange("q (t r) -> q r t", t=PLANES),
+                scalar=iw[:, 1:2],
+                in1=field_terms[b][:].rearrange("q (t i r) -> q i r t", t=PLANES, i=TILES)[:, i],
+                op0=ALU.mult,
+                op1=ALU.add,
+            )
 
         def quantise_enhanced(b):
             codes = work.tile([P, N], U32, tag="e_codes", align_bytes=64)
@@ -382,41 +379,63 @@ def tile_fieldinteractionoperators_pa_t_kernel(
             e_codes[b] = codes
             e_scales[b] = scales
 
-        def second_product_and_store(b):
-            result = rows_out.tile([P, TILES * D], F32, tag="result")
-            for i in range(TILES):
-                tokens = slice(i * P, (i + 1) * P)
-                columns = slice(i * D, (i + 1) * D)
-                projected = products.tile([P, D], F32, tag="product")
-                nc.tensor.matmul_mx(
-                    out=projected[:],
-                    lhsT=e_codes[b][:, tokens].bitcast(FP8X4),
-                    lhsT_scale=e_scales[b][:, tokens],
-                    rhs=out_w_codes[:].bitcast(FP8X4),
-                    rhs_scale=out_w_scales[:],
-                    start=True,
-                    stop=True,
+        def second_product(b, i):
+            if i == 0:
+                result = rows_out.tile([P, TILES * D], F32, tag="result")
+                results[b] = result
+            tokens = slice(i * P, (i + 1) * P)
+            columns = slice(i * D, (i + 1) * D)
+            projected = products.tile([P, D], F32, tag="product")
+            nc.tensor.matmul_mx(
+                out=projected[:],
+                lhsT=e_codes[b][:, tokens].bitcast(FP8X4),
+                lhsT_scale=e_scales[b][:, tokens],
+                rhs=out_w_codes[:].bitcast(FP8X4),
+                rhs_scale=out_w_scales[:],
+                start=True,
+                stop=True,
+            )
+            if i < OUT_TILES_ON_SCALAR:
+                nc.scalar.copy(out=results[b][:, columns], in_=projected[:])
+                nc.gpsimd.tensor_tensor(
+                    out=results[b][:, columns], in0=results[b][:, columns], in1=out_bias[:], op=ALU.add
                 )
-                if i < OUT_TILES_ON_VECTOR:
-                    nc.vector.tensor_tensor(out=result[:, columns], in0=projected[:], in1=out_bias[:], op=ALU.add)
-                else:
-                    nc.scalar.copy(out=result[:, columns], in_=projected[:])
-                    nc.gpsimd.tensor_tensor(out=result[:, columns], in0=result[:, columns], in1=out_bias[:], op=ALU.add)
-            nc.sync.dma_start(out=out[b].rearrange("(p i) o -> p (i o)", i=TILES), in_=result[:])
+            else:
+                nc.vector.tensor_tensor(out=results[b][:, columns], in0=projected[:], in1=out_bias[:], op=ALU.add)
 
-        for j in range(-2, B + 1):
-            if 0 <= j and j + LOADS_AHEAD < B:
+        def store(b):
+            nc.sync.dma_start(out=out[b].rearrange("(p i) o -> p (i o)", i=TILES), in_=results[b][:])
+
+        def entry(b):
+            return 0 <= b < B
+
+        for j in range(-LOADS_AHEAD, B + 1):
+            if entry(j + LOADS_AHEAD):
                 load(j + LOADS_AHEAD)
-            if 0 <= j + 1 < B:
-                field_scales_products(j + 1)
+            if entry(j - 1):
+                for i in range(OUT_TILES_ON_SCALAR):
+                    second_product(j - 1, i)
+            if entry(j + 2):
+                field_scales_products(j + 2)
+            if entry(j + 1):
                 quantise_h(j + 1)
-                field_scales_sums(j + 1)
-                field_term(j + 1)
-            if 0 <= j < B:
-                first_product_and_fusion(j)
-            if 0 <= j - 1 < B:
-                second_product_and_store(j - 1)
-            if 0 <= j < B:
+            if entry(j + 2):
+                field_scales_sums(j + 2)
+            for i in range(TILES):
+                if entry(j):
+                    first_product_and_fusion(j, i)
+                if entry(j + 2):
+                    if i < TILES // 2:
+                        transpose_h(j + 2, i)
+                    else:
+                        transpose_fields(j + 2, i - TILES // 2)
+            if entry(j + 2):
+                last_rows(j + 2)
+            if entry(j - 1):
+                for i in range(OUT_TILES_ON_SCALAR, TILES):
+                    second_product(j - 1, i)
+                store(j - 1)
+            if entry(j):
                 quantise_enhanced(j)
-            if 0 <= j + 2 < B:
-                transposes(j + 2)
+            if entry(j + 3):
+                total_fields(j + 3)

@@ -409,12 +409,12 @@ def tile_fieldinteractionoperators_pa_t_kernel(
         def entry(b):
             return 0 <= b < B
 
-        for j in range(-LOADS_AHEAD, B + 1):
+        for j in range(-LOADS_AHEAD, B + 2):
             if entry(j + LOADS_AHEAD):
                 load(j + LOADS_AHEAD)
-            if entry(j - 1):
+            if entry(j - 2):
                 for i in range(OUT_TILES_ON_SCALAR):
-                    second_product(j - 1, i)
+                    second_product(j - 2, i)
             if entry(j + 2):
                 field_scales_products(j + 2)
             if entry(j + 1):
@@ -431,10 +431,10 @@ def tile_fieldinteractionoperators_pa_t_kernel(
                         transpose_fields(j + 2, i - TILES // 2)
             if entry(j + 2):
                 last_rows(j + 2)
-            if entry(j - 1):
+            if entry(j - 2):
                 for i in range(OUT_TILES_ON_SCALAR, TILES):
-                    second_product(j - 1, i)
-                store(j - 1)
+                    second_product(j - 2, i)
+                store(j - 2)
             if entry(j):
                 quantise_enhanced(j)
             if entry(j + 3):

@@ -258,6 +258,7 @@ def tile_fieldinteractionoperators_pa_t_kernel(
         h_scales = {}
         field_totals = {}
         field_terms = {}
+        last_scaled = {}
         enhanced = {}
         e_codes = {}
         e_scales = {}
@@ -323,18 +324,20 @@ def tile_fieldinteractionoperators_pa_t_kernel(
                 op=ALU.add,
             )
 
-        def last_rows(b):
-            term = field_terms[b]
-            last_scaled = work.tile([P, SCALES], F32, tag="last_scaled")
+        def scale_last_rows(b):
+            scaled = work.tile([P, SCALES], F32, tag="last_scaled")
             nc.gpsimd.tensor_tensor(
-                out=last_scaled[:],
+                out=scaled[:],
                 in0=last_tokens[:, b * SCALES : (b + 1) * SCALES],
                 in1=scales_all[:, b * SCALES : (b + 1) * SCALES],
                 op=ALU.mult,
             )
+            last_scaled[b] = scaled
+
+        def write_last_rows(b):
             nc.gpsimd.tensor_tensor(
-                out=term[:].rearrange("q (t i r) -> q i t r", t=PLANES, i=TILES)[:, :, :, P - 1],
-                in0=last_scaled[:].rearrange("q (i t) -> q i t", i=TILES),
+                out=field_terms[b][:].rearrange("q (t i r) -> q i t r", t=PLANES, i=TILES)[:, :, :, P - 1],
+                in0=last_scaled[b][:].rearrange("q (i t) -> q i t", i=TILES),
                 in1=nl_bias[:].unsqueeze(1).to_broadcast([P, TILES, PLANES]),
                 op=ALU.add,
             )
@@ -412,15 +415,16 @@ def tile_fieldinteractionoperators_pa_t_kernel(
         for j in range(-LOADS_AHEAD, B + 2):
             if entry(j + LOADS_AHEAD):
                 load(j + LOADS_AHEAD)
-            if entry(j - 2):
-                for i in range(OUT_TILES_ON_SCALAR):
-                    second_product(j - 2, i)
             if entry(j + 2):
                 field_scales_products(j + 2)
             if entry(j + 1):
                 quantise_h(j + 1)
             if entry(j + 2):
                 field_scales_sums(j + 2)
+                scale_last_rows(j + 2)
+            if entry(j - 2):
+                for i in range(OUT_TILES_ON_SCALAR):
+                    second_product(j - 2, i)
             for i in range(TILES):
                 if entry(j):
                     first_product_and_fusion(j, i)
@@ -430,7 +434,7 @@ def tile_fieldinteractionoperators_pa_t_kernel(
                     else:
                         transpose_fields(j + 2, i - TILES // 2)
             if entry(j + 2):
-                last_rows(j + 2)
+                write_last_rows(j + 2)
             if entry(j - 2):
                 for i in range(OUT_TILES_ON_SCALAR, TILES):
                     second_product(j - 2, i)

@@ -17,19 +17,20 @@ B = 16
 N = 512
 D = 512
 HEADS = 8
-HEAD_DIM = D // HEADS
 LAGS = 3
 TILES = N // P
 PLANES = 4
 HALVES = 2
 ROW = TILES * D
+BANK = 512
 KERNEL_CHANNELS = 4
 SUMS = HEADS * KERNEL_CHANNELS
+CANDIDATES = 8
+SLOTS = CANDIDATES + LAGS + 1
 SCALES = TILES * PLANES
-HELD = 9
-WEIGHTED = (TILES - 1) * PLANES * HELD
-LOADS_AHEAD = 5
-ROW_BUFFERS = 4
+TERMS = (TILES - 1) * PLANES * SLOTS
+PRELOADED = 3
+LOADS_AHEAD = 4
 OUT_TILES_ON_SCALAR = 2
 
 FLOPS = 2 * 2 * B * N * D * D
@@ -42,10 +43,8 @@ def tile_fieldinteractionoperators_pa_t_kernel(
     with ExitStack() as ctx:
         ctx.enter_context(tc.manual_schedule())
         const = ctx.enter_context(tc.tile_pool(name="const", bufs=1))
-        rows_in = ctx.enter_context(tc.tile_pool(name="rows_in", bufs=ROW_BUFFERS))
-        weights_in = ctx.enter_context(tc.tile_pool(name="weights_in", bufs=2))
+        rows_in = ctx.enter_context(tc.tile_pool(name="rows_in", bufs=LOADS_AHEAD))
         work = ctx.enter_context(tc.tile_pool(name="work", bufs=2))
-        terms = ctx.enter_context(tc.tile_pool(name="terms", bufs=3))
         rows_out = ctx.enter_context(tc.tile_pool(name="rows_out", bufs=3))
         transposed = ctx.enter_context(tc.psum_pool(name="transposed", bufs=3))
         products = ctx.enter_context(tc.psum_pool(name="products", bufs=4))
@@ -53,41 +52,38 @@ def tile_fieldinteractionoperators_pa_t_kernel(
 
         identity = const.tile([P, P], F32)
         make_identity(nc, identity[:])
-        vector_rows = const.tile([P, 768], BF16)
-        nc.vector.memset(vector_rows[:], 0.0)
-        b3_rows = const.tile([P, D // HALVES], BF16)
-        nc.vector.memset(b3_rows[:], 0.0)
-        edge_rows = const.tile([P, ROW], BF16)
-        nc.vector.memset(edge_rows[:], 0.0)
-        ones = const.tile([P, P], BF16)
-        nc.vector.memset(ones[:], 1.0)
+        terms_all = const.tile([P, B * TERMS], F32)
+        nc.gpsimd.memset(terms_all[:], 0.0)
+
         zero_column = const.tile([P, 1], F32)
         nc.vector.memset(zero_column[:], 0.0)
-        lag_weight = const.tile([P, LAGS * SUMS], F32)
-        nc.vector.memset(lag_weight[:], 0.0)
+        edge_rows = const.tile([P, ROW], BF16)
+        nc.vector.memset(edge_rows[32:64, :], 0.0)
+        nc.vector.memset(edge_rows[64:P, :], 0.0)
+        out_b_rows = const.tile([P, D], BF16)
+        nc.vector.memset(out_b_rows[:], 0.0)
+        ones = const.tile([P, P], BF16)
+        nc.vector.memset(ones[:], 1.0)
         scales_all = const.tile([P, B * SCALES], F32)
         nc.vector.memset(scales_all[:], 1.0)
+        weights = const.tile([P, (LAGS + 2) * SUMS], F32)
+        nc.vector.memset(weights[:], 0.0)
 
-        nc.scalar.dma_start(out=vector_rows[0:1, 640:642], in_=inter_w.rearrange("(o c) -> o c", o=1))
-        nc.scalar.dma_start(
-            out=vector_rows[0:1, 512:584], in_=corr_kernels.rearrange("(o h) l j -> o (h l j)", o=1)
+        logits = const.tile([P, 2], BF16)
+        nc.sync.dma_start(out=logits[:], in_=inter_w.partition_broadcast(P))
+        kernels = const.tile([P, HEADS * LAGS * LAGS], BF16)
+        nc.sync.dma_start(out=kernels[:], in_=corr_kernels.rearrange("h l j -> (h l j)").partition_broadcast(P))
+        nc.sync.dma_start(out=edge_rows[0:B, :], in_=fields[:, 0:TILES, :].rearrange("b n c -> b (n c)"))
+        nc.sync.dma_start(out=edge_rows[B : 2 * B, :], in_=fields[:, N - TILES : N, :].rearrange("b n c -> b (n c)"))
+        b3_planes = const.tile([P, PLANES], BF16)
+        nc.sync.dma_start(
+            out=b3_planes[:].rearrange("q (u e) -> q u e", e=2), in_=b3.rearrange("(u q e) -> q u e", u=HALVES, e=2)
         )
-        nc.scalar.dma_start(out=edge_rows[0:B, :], in_=fields[:, 0:TILES, :].rearrange("b n c -> b (n c)"))
-        nc.scalar.dma_start(
-            out=edge_rows[B : 2 * B, :], in_=fields[:, N - TILES : N, :].rearrange("b n c -> b (n c)")
-        )
-        nc.scalar.dma_start(out=b3_rows[0:HALVES, :], in_=b3.rearrange("(u c) -> u c", u=HALVES))
-        nc.scalar.dma_start(out=vector_rows[0:1, 0:D], in_=out_b.rearrange("(o c) -> o c", o=1))
 
-        w3_rows = weights_in.tile([P, ROW], BF16, tag="weight_rows")
+        w3_rows = const.tile([P, ROW], BF16)
         nc.sync.dma_start(
             out=w3_rows[:].rearrange("m (u x) -> m u x", u=HALVES),
             in_=w3.rearrange("(u m e) k -> m u (e k)", u=HALVES, e=2),
-        )
-        out_w_rows = weights_in.tile([P, ROW], BF16, tag="weight_rows")
-        nc.sync.dma_start(
-            out=out_w_rows[:].rearrange("m (a k) -> m a k", a=TILES),
-            in_=out_w.rearrange("(a m) k -> m a k", a=TILES),
         )
 
         h_rows = {}
@@ -101,10 +97,19 @@ def tile_fieldinteractionoperators_pa_t_kernel(
             nc.sync.dma_start(out=f_tile[:], in_=fields[b].rearrange("(p i) c -> p (i c)", i=TILES))
             f_rows[b] = f_tile
 
+        for b in range(PRELOADED):
+            load(b)
+        out_w_rows = const.tile([P, ROW], BF16)
+        nc.sync.dma_start(
+            out=out_w_rows[:].rearrange("m (a k) -> m a k", a=TILES),
+            in_=out_w.rearrange("(a m) k -> m a k", a=TILES),
+        )
+        nc.sync.dma_start(out=out_b_rows[0:1, :], in_=out_b.rearrange("(o c) -> o c", o=1))
+
         def rows_to_words(rows, grouped, pair):
             words = rows[:].bitcast(F32)
             grouped_words = grouped[:].bitcast(F32)
-            bank = transposed.tile([P, 512], F32, tag="words")
+            bank = transposed.tile([P, BANK], F32, tag="words")
             for k in range(2):
                 for u in range(HALVES):
                     first = (2 * pair + k) * (D // 2) + u * P
@@ -114,24 +119,42 @@ def tile_fieldinteractionoperators_pa_t_kernel(
                         identity[:],
                     )
             nc.scalar.copy(
-                out=grouped_words[:, pair * 512 : (pair + 1) * 512].rearrange("q (k r u) -> q k r u", k=2, u=HALVES),
+                out=grouped_words[:, pair * BANK : (pair + 1) * BANK].rearrange("q (k r u) -> q k r u", k=2, u=HALVES),
                 in_=bank[:].rearrange("q (k u r) -> q k r u", k=2, u=HALVES),
             )
 
         def quantise(grouped, codes, scales):
             nc.vector.quantize_mx(out=codes[:].bitcast(FP8X4), scales=scales[:], in_=grouped[:])
 
+        def prepare_weight(rows, codes, scales):
+            grouped = work.tile([P, PLANES * D], BF16, tag="weight_grouped", bufs=1, align_bytes=64)
+            for pair in range(TILES // 2):
+                rows_to_words(rows, grouped, pair)
+            quantise(grouped, codes, scales)
+
+
+        norm = const.tile([P, LAGS * SUMS], F32)
+        lives_here = identity[:].rearrange("p (g x) -> p g x", x=32)[:, :, 0:2].unsqueeze(1)
+        for lag in range(1, LAGS + 1):
+            for e in range(2):
+                nc.vector.tensor_scalar_mul(
+                    out=norm[:].rearrange("p (l u g r e) -> p l u g r e", l=LAGS, u=HALVES, g=4, e=2)[
+                        :, lag - 1, :, :, :, e
+                    ],
+                    in0=lives_here.to_broadcast([P, HALVES, 4, 2]),
+                    scalar1=1.0 / (LAGS * (N - lag)),
+                )
+
         warm = const.tile([P, 1], F32)
         nc.scalar.activation(out=warm[:], in_=zero_column[:], func=ACT.Exp)
 
-        spread_small_ps = products.tile([P, 512], F32, tag="product")
-        nc.tensor.matmul(
-            out=spread_small_ps[:, 0:256], lhsT=ones[:], rhs=vector_rows[:, 512:768], start=True, stop=True
+        own = weights[:, 2 * SUMS :]
+        nc.vector.tensor_tensor(
+            out=own.rearrange("p (l h j) -> p l h j", l=LAGS, h=HEADS)[:, :, :, 0:LAGS],
+            in0=kernels[:].rearrange("p (h l j) -> p l h j", h=HEADS, l=LAGS),
+            in1=norm[:].rearrange("p (l h j) -> p l h j", l=LAGS, h=HEADS)[:, :, :, 0:LAGS],
+            op=ALU.mult,
         )
-        spread_small = const.tile([P, 256], F32)
-        nc.vector.tensor_copy(out=spread_small[:], in_=spread_small_ps[:, 0:256])
-
-        logits = spread_small[:, 128:130]
         top = const.tile([P, 1], F32)
         nc.vector.tensor_tensor(out=top[:], in0=logits[:, 0:1], in1=logits[:, 1:2], op=ALU.max)
         minus_top = const.tile([P, 1], F32)
@@ -139,119 +162,83 @@ def tile_fieldinteractionoperators_pa_t_kernel(
         exps = const.tile([P, 2], F32)
         exp_sum = const.tile([P, 1], F32)
         nc.scalar.activation(
-            out=exps[:], in_=logits, func=ACT.Exp, bias=minus_top[:, 0:1], scale=1.0, accum_out=exp_sum[:, 0:1]
+            out=exps[:], in_=logits[:], func=ACT.Exp, bias=minus_top[:, 0:1], scale=1.0, accum_out=exp_sum[:, 0:1]
         )
-        inv_sum = const.tile([P, 1], F32)
-        nc.vector.reciprocal(out=inv_sum[:], in_=exp_sum[:])
-        iw = const.tile([P, 2], F32)
-        nc.vector.tensor_scalar_mul(out=iw[:], in0=exps[:], scalar1=inv_sum[:, 0:1])
+        for block in (1, 0):
+            nc.vector.tensor_tensor(
+                out=weights[:, block * SUMS : (block + 1) * SUMS],
+                in0=weights[:, (block + 1) * SUMS : (block + 2) * SUMS],
+                in1=weights[:, (4 - block) * SUMS : (5 - block) * SUMS],
+                op=ALU.add,
+            )
+        plane_weight = const.tile([P, PLANES * LAGS], F32)
+        for u in range(HALVES):
+            nc.vector.tensor_reduce(
+                out=plane_weight[:, u * 2 * LAGS : (u + 1) * 2 * LAGS].rearrange("p (l e) -> p l e", e=2),
+                in_=own.rearrange("p (l u m e) -> p u l e m", l=LAGS, u=HALVES, e=2)[:, u],
+                axis=AXIS.X,
+                op=ALU.add,
+            )
 
-        b3_ps = products.tile([P, 512], F32, tag="product")
-        nc.tensor.transpose(b3_ps[:, 0:P], b3_rows[:].bitcast(F32), identity[:])
-        nl_bias = const.tile([P, PLANES], F32)
-        nc.vector.tensor_scalar_mul(out=nl_bias[:], in0=b3_ps[:, 0:HALVES].bitcast(BF16), scalar1=iw[:, 1:2])
-
-        out_bias_ps = products.tile([P, 512], F32, tag="product")
-        nc.tensor.matmul(out=out_bias_ps[:], lhsT=ones[:], rhs=vector_rows[:, 0:D], start=True, stop=True)
-        out_bias = const.tile([P, D], F32)
-        nc.vector.tensor_copy(out=out_bias[:], in_=out_bias_ps[:])
-
-        first_tokens = const.tile([P, B * SCALES], F32)
+        heads = const.tile([P, B * PLANES * LAGS], F32)
         last_tokens = const.tile([P, B * SCALES], F32)
         edge_words = edge_rows[:].bitcast(F32)
         for u in range(HALVES):
-            edge_bank = transposed.tile([P, 512], F32, tag="words")
+            edge_bank = transposed.tile([P, BANK], F32, tag="words")
             for n in range(TILES):
                 first = n * (D // 2) + u * P
                 nc.tensor.transpose(edge_bank[:, n * P : (n + 1) * P], edge_words[:, first : first + P], identity[:])
             edge_values = edge_bank[:].bitcast(BF16).rearrange("q (n c e) -> q n c e", n=TILES, e=2)
-            for tokens, first_row in ((first_tokens, 0), (last_tokens, B)):
-                nc.vector.tensor_copy(
-                    out=tokens[:].rearrange("q (b n u e) -> q n b u e", b=B, n=TILES, e=2)[:, :, :, u, :],
-                    in_=edge_values[:, :, first_row : first_row + B, :],
-                )
-
-        w3_grouped = work.tile([P, PLANES * 512], BF16, tag="row_grouped", align_bytes=64)
-        out_w_grouped = work.tile([P, PLANES * 512], BF16, tag="row_grouped", align_bytes=64)
-        for pair in range(TILES // 2):
-            rows_to_words(w3_rows, w3_grouped, pair)
-        for pair in range(TILES // 2):
-            rows_to_words(out_w_rows, out_w_grouped, pair)
-
-        kernels = spread_small[:, 0:72].rearrange("p (h l j) -> p l h j", h=HEADS, l=LAGS)
-        lag_weight_hj = lag_weight[:].rearrange("p (l h j) -> p l h j", l=LAGS, h=HEADS)
-        for lag in range(1, LAGS + 1):
-            nc.vector.tensor_scalar(
-                out=lag_weight_hj[:, lag - 1, :, 0:LAGS],
-                in0=kernels[:, lag - 1],
-                scalar1=iw[:, 0:1],
-                scalar2=1.0 / (LAGS * (N - lag)),
-                op0=ALU.mult,
-                op1=ALU.mult,
+            nc.vector.tensor_copy(
+                out=heads[:].rearrange("q (b u n e) -> q n b u e", b=B, u=HALVES, e=2)[:, :, :, u, :],
+                in_=edge_values[:, 0:LAGS, 0:B, :],
             )
-        own_weight = const.tile([P, LAGS * SUMS], F32)
-        lives_here = identity[:].rearrange("p (g x) -> p g x", x=32)[:, :, 0:2].unsqueeze(1)
-        for e in range(2):
+            nc.vector.tensor_copy(
+                out=last_tokens[:].rearrange("q (b n u e) -> q n b u e", b=B, n=TILES, e=2)[:, :, :, u, :],
+                in_=edge_values[:, :, B : 2 * B, :],
+            )
+        heads_bune = heads[:].rearrange("q (b u n e) -> q b u n e", b=B, u=HALVES, e=2)
+        for n in range(1, LAGS):
             nc.vector.tensor_tensor(
-                out=own_weight[:].rearrange("p (a g r e) -> p a g r e", g=4, r=2, e=2)[:, :, :, :, e],
-                in0=lag_weight[:].rearrange("p (a g r e) -> p a g r e", g=4, r=2, e=2)[:, :, :, :, e],
-                in1=lives_here.to_broadcast([P, LAGS * HALVES, 4, 2]),
-                op=ALU.mult,
+                out=heads_bune[:, :, :, n, :], in0=heads_bune[:, :, :, n, :], in1=heads_bune[:, :, :, n - 1, :], op=ALU.add
             )
-        plane_weight = const.tile([P, LAGS * PLANES], F32)
-        nc.vector.tensor_reduce(
-            out=plane_weight[:].rearrange("p (a e) -> p a e", e=2),
-            in_=own_weight[:].rearrange("p (a m e) -> p a e m", m=8, e=2),
-            axis=AXIS.X,
-            op=ALU.add,
-        )
+
+        inv_sum = const.tile([P, 1], F32)
+        nc.vector.reciprocal(out=inv_sum[:], in_=exp_sum[:])
+        iw = const.tile([P, 2], F32)
+        nc.vector.tensor_scalar_mul(out=iw[:], in0=exps[:], scalar1=inv_sum[:, 0:1])
+        minus_iw0 = const.tile([P, 1], F32)
+        nc.vector.tensor_scalar_mul(out=minus_iw0[:], in0=iw[:, 0:1], scalar1=-1.0)
         total_weight = const.tile([P, (TILES - 1) * SUMS], F32)
-        for lag in range(1, LAGS + 1):
-            i = LAGS - lag
-            if lag == 1:
-                nc.vector.tensor_copy(
-                    out=total_weight[:, i * SUMS : (i + 1) * SUMS], in_=own_weight[:, 0:SUMS]
-                )
-            else:
-                nc.vector.tensor_tensor(
-                    out=total_weight[:, i * SUMS : (i + 1) * SUMS],
-                    in0=total_weight[:, (i + 1) * SUMS : (i + 2) * SUMS],
-                    in1=own_weight[:, (lag - 1) * SUMS : lag * SUMS],
-                    op=ALU.add,
-                )
-
-        weighted_all = const.tile([P, B * WEIGHTED], F32)
-        held = weighted_all[:].rearrange("q (b i u m e) -> q b i u m e", b=B, i=TILES - 1, u=HALVES, e=2)
-        scales_bite = scales_all[:].rearrange("q (b i u e) -> q b i u e", b=B, i=TILES, e=2)
-        first_bnue = first_tokens[:].rearrange("q (b n u e) -> q b n u e", b=B, n=TILES, e=2)
-        head = first_bnue[:, :, 0]
-        for lag in range(1, LAGS + 1):
-            i = LAGS - lag
-            if lag > 1:
-                longer = const.tile([P, B * PLANES], F32, name="head%d" % lag)
-                longer_bue = longer[:].rearrange("q (b u e) -> q b u e", b=B, e=2)
-                nc.vector.tensor_tensor(out=longer_bue, in0=head, in1=first_bnue[:, :, lag - 1], op=ALU.add)
-                head = longer_bue
-            head_term = const.tile([P, B * PLANES], F32, name="head_term%d" % lag)
-            head_term_bue = head_term[:].rearrange("q (b u e) -> q b u e", b=B, e=2)
+        nc.vector.tensor_scalar_mul(out=total_weight[:], in0=weights[:, 0 : (TILES - 1) * SUMS], scalar1=iw[:, 0:1])
+        head_weight = const.tile([P, PLANES * LAGS], F32)
+        nc.vector.tensor_scalar_mul(out=head_weight[:], in0=plane_weight[:], scalar1=minus_iw0[:, 0:1])
+        nc.vector.memset(terms_all[:].rearrange("q (a m e) -> q a m e", m=SLOTS, e=2)[:, :, SLOTS - 1, :], 1.0)
+        for i in range(TILES - 1):
+            counted = 2 * (LAGS - i)
             nc.vector.tensor_tensor(
-                out=head_term_bue,
-                in0=head,
-                in1=plane_weight[:, (lag - 1) * PLANES : lag * PLANES]
-                .rearrange("q (u e) -> q u e", e=2)
+                out=terms_all[:].rearrange("q (b i u x) -> q b i u x", b=B, i=TILES - 1, u=HALVES)[
+                    :, :, i, :, 2 * CANDIDATES : 2 * CANDIDATES + counted
+                ],
+                in0=heads[:].rearrange("q (b u x) -> q b u x", b=B, u=HALVES)[:, :, :, 0:counted],
+                in1=head_weight[:]
+                .rearrange("q (u x) -> q u x", u=HALVES)[:, :, 0:counted]
                 .unsqueeze(1)
-                .to_broadcast([P, B, HALVES, 2]),
+                .to_broadcast([P, B, HALVES, counted]),
                 op=ALU.mult,
             )
-            before = scales_bite[:, :, TILES - 1] if lag == 1 else held[:, :, i + 1, :, HELD - 1, :]
-            nc.vector.tensor_tensor(out=held[:, :, i, :, HELD - 1, :], in0=before, in1=head_term_bue, op=ALU.subtract)
+
+        nl_bias = const.tile([P, PLANES], F32)
+        nc.vector.tensor_scalar_mul(out=nl_bias[:], in0=b3_planes[:], scalar1=iw[:, 1:2])
 
         w3_codes = const.tile([P, D], U32, align_bytes=64)
         w3_scales = const.tile([P, D], U8, align_bytes=64)
-        quantise(w3_grouped, w3_codes, w3_scales)
-        out_w_codes = const.tile([P, D], U32, align_bytes=64)
-        out_w_scales = const.tile([P, D], U8, align_bytes=64)
-        quantise(out_w_grouped, out_w_codes, out_w_scales)
+        prepare_weight(w3_rows, w3_codes, w3_scales)
+
+        out_bias_ps = products.tile([P, BANK], F32, tag="product")
+        nc.tensor.matmul(out=out_bias_ps[:], lhsT=ones[:], rhs=out_b_rows[:], start=True, stop=True)
+        out_bias = const.tile([P, D], F32)
+        nc.vector.tensor_copy(out=out_bias[:], in_=out_bias_ps[:])
 
         h_grouped = {}
         h_codes = {}
@@ -263,6 +250,8 @@ def tile_fieldinteractionoperators_pa_t_kernel(
         e_codes = {}
         e_scales = {}
         results = {}
+        out_w_codes = const.tile([P, D], U32, align_bytes=64)
+        out_w_scales = const.tile([P, D], U8, align_bytes=64)
 
         def total_fields(b):
             total = totals.tile([P, SUMS], F32, tag="total")
@@ -277,41 +266,15 @@ def tile_fieldinteractionoperators_pa_t_kernel(
                 )
             field_totals[b] = total
 
-        def transpose_h(b, pair):
-            if pair == 0:
-                grouped = work.tile([P, PLANES * N], BF16, tag="row_grouped", align_bytes=64)
-                h_grouped[b] = grouped
-            rows_to_words(h_rows[b], h_grouped[b], pair)
-
-        def transpose_fields(b, u):
-            if u == 0:
-                term = terms.tile([P, PLANES * N], F32, tag="field_term")
-                field_terms[b] = term
-            f_words = f_rows[b][:].bitcast(F32)
-            bank = transposed.tile([P, N], F32, tag="words")
-            for i in range(TILES):
-                first = i * (D // 2) + u * P
-                nc.tensor.transpose(bank[:, i * P : (i + 1) * P], f_words[:, first : first + P], identity[:])
-            values = bank[:].bitcast(BF16).rearrange("q (x e) -> q x e", e=2)
-            for e in range(2):
-                t = 2 * u + e
-                nc.scalar.activation(
-                    out=field_terms[b][:, t * N : (t + 1) * N],
-                    in_=values[:, :, e],
-                    func=ACT.Identity,
-                    bias=nl_bias[:, t : t + 1],
-                    scale=scales_all[:, b * SCALES + t : b * SCALES + t + 1],
-                )
-
         def field_scales_products(b):
             nc.vector.tensor_tensor(
-                out=weighted_all[:, b * WEIGHTED : (b + 1) * WEIGHTED].rearrange(
-                    "q (i u x) -> q i u x", i=TILES - 1, u=HALVES
-                )[:, :, :, 0:16],
+                out=terms_all[:, b * TERMS : (b + 1) * TERMS].rearrange("q (i u x) -> q i u x", i=TILES - 1, u=HALVES)[
+                    :, :, :, 0 : 2 * CANDIDATES
+                ],
                 in0=field_totals[b][:]
                 .rearrange("q (u x) -> q u x", u=HALVES)
                 .unsqueeze(1)
-                .to_broadcast([P, TILES - 1, HALVES, 16]),
+                .to_broadcast([P, TILES - 1, HALVES, 2 * CANDIDATES]),
                 in1=total_weight[:].rearrange("q (i u x) -> q i u x", i=TILES - 1, u=HALVES),
                 op=ALU.mult,
             )
@@ -319,7 +282,7 @@ def tile_fieldinteractionoperators_pa_t_kernel(
         def field_scales_sums(b):
             nc.vector.tensor_reduce(
                 out=scales_all[:, b * SCALES : b * SCALES + (TILES - 1) * PLANES].rearrange("q (a e) -> q a e", e=2),
-                in_=weighted_all[:, b * WEIGHTED : (b + 1) * WEIGHTED].rearrange("q (a m e) -> q a e m", m=HELD, e=2),
+                in_=terms_all[:, b * TERMS : (b + 1) * TERMS].rearrange("q (a m e) -> q a e m", m=SLOTS, e=2),
                 axis=AXIS.X,
                 op=ALU.add,
             )
@@ -342,6 +305,32 @@ def tile_fieldinteractionoperators_pa_t_kernel(
                 op=ALU.add,
             )
 
+        def transpose_h(b, pair):
+            if pair == 0:
+                grouped = work.tile([P, PLANES * N], BF16, tag="h_grouped", align_bytes=64)
+                h_grouped[b] = grouped
+            rows_to_words(h_rows[b], h_grouped[b], pair)
+
+        def transpose_fields(b, u):
+            if u == 0:
+                term = work.tile([P, PLANES * N], F32, tag="field_term")
+                field_terms[b] = term
+            f_words = f_rows[b][:].bitcast(F32)
+            bank = transposed.tile([P, BANK], F32, tag="words")
+            for i in range(TILES):
+                first = i * (D // 2) + u * P
+                nc.tensor.transpose(bank[:, i * P : (i + 1) * P], f_words[:, first : first + P], identity[:])
+            values = bank[:].bitcast(BF16).rearrange("q (x e) -> q x e", e=2)
+            for e in range(2):
+                t = 2 * u + e
+                nc.scalar.activation(
+                    out=field_terms[b][:, t * N : (t + 1) * N],
+                    in_=values[:, :, e],
+                    func=ACT.Identity,
+                    bias=nl_bias[:, t : t + 1],
+                    scale=scales_all[:, b * SCALES + t : b * SCALES + t + 1],
+                )
+
         def quantise_h(b):
             codes = work.tile([P, N], U32, tag="h_codes", align_bytes=64)
             scales = work.tile([P, N], U8, tag="h_scales", align_bytes=64)
@@ -354,7 +343,7 @@ def tile_fieldinteractionoperators_pa_t_kernel(
                 fused = work.tile([P, PLANES * N], BF16, tag="enhanced", align_bytes=64)
                 enhanced[b] = fused
             tokens = slice(i * P, (i + 1) * P)
-            nl = products.tile([P, PLANES * P], F32, tag="product")
+            nl = products.tile([P, BANK], F32, tag="product")
             for t in range(PLANES):
                 channels = slice(t * P, (t + 1) * P)
                 nc.tensor.matmul_mx(
@@ -367,7 +356,7 @@ def tile_fieldinteractionoperators_pa_t_kernel(
                     stop=True,
                 )
             nc.vector.scalar_tensor_tensor(
-                out=enhanced[b][:, i * PLANES * P : (i + 1) * PLANES * P].rearrange("q (r t) -> q r t", t=PLANES),
+                out=enhanced[b][:, i * BANK : (i + 1) * BANK].rearrange("q (r t) -> q r t", t=PLANES),
                 in0=nl[:].rearrange("q (t r) -> q r t", t=PLANES),
                 scalar=iw[:, 1:2],
                 in1=field_terms[b][:].rearrange("q (t i r) -> q i r t", t=PLANES, i=TILES)[:, i],
@@ -382,13 +371,13 @@ def tile_fieldinteractionoperators_pa_t_kernel(
             e_codes[b] = codes
             e_scales[b] = scales
 
-        def second_product(b, i):
+        def second_product_and_store(b, i, on_scalar):
             if i == 0:
                 result = rows_out.tile([P, TILES * D], F32, tag="result")
                 results[b] = result
             tokens = slice(i * P, (i + 1) * P)
             columns = slice(i * D, (i + 1) * D)
-            projected = products.tile([P, D], F32, tag="product")
+            projected = products.tile([P, BANK], F32, tag="product")
             nc.tensor.matmul_mx(
                 out=projected[:],
                 lhsT=e_codes[b][:, tokens].bitcast(FP8X4),
@@ -398,48 +387,52 @@ def tile_fieldinteractionoperators_pa_t_kernel(
                 start=True,
                 stop=True,
             )
-            if i < OUT_TILES_ON_SCALAR:
+            if on_scalar:
                 nc.scalar.copy(out=results[b][:, columns], in_=projected[:])
                 nc.gpsimd.tensor_tensor(
                     out=results[b][:, columns], in0=results[b][:, columns], in1=out_bias[:], op=ALU.add
                 )
             else:
                 nc.vector.tensor_tensor(out=results[b][:, columns], in0=projected[:], in1=out_bias[:], op=ALU.add)
-
-        def store(b):
-            nc.sync.dma_start(out=out[b].rearrange("(p i) o -> p (i o)", i=TILES), in_=results[b][:])
+            if i % 2 == 1:
+                pair = slice((i - 1) * D, (i + 1) * D)
+                nc.sync.dma_start(out=out[b].rearrange("(p i) o -> p (i o)", i=TILES)[:, pair], in_=results[b][:, pair])
 
         def entry(b):
             return 0 <= b < B
 
-        for j in range(-LOADS_AHEAD, B + 2):
-            if entry(j + LOADS_AHEAD):
+        def step(j):
+            if PRELOADED <= j + LOADS_AHEAD < B:
                 load(j + LOADS_AHEAD)
-            if entry(j + 2):
-                field_scales_products(j + 2)
             if entry(j + 1):
+                field_scales_products(j + 1)
                 quantise_h(j + 1)
-            if entry(j + 2):
-                field_scales_sums(j + 2)
-                scale_last_rows(j + 2)
+                field_scales_sums(j + 1)
+                scale_last_rows(j + 1)
+            tiles_on_scalar = OUT_TILES_ON_SCALAR if entry(j) else 0
             if entry(j - 2):
-                for i in range(OUT_TILES_ON_SCALAR):
-                    second_product(j - 2, i)
+                for i in range(tiles_on_scalar):
+                    second_product_and_store(j - 2, i, True)
             for i in range(TILES):
                 if entry(j):
                     first_product_and_fusion(j, i)
-                if entry(j + 2):
-                    if i < TILES // 2:
+                if i < TILES // 2:
+                    if entry(j + 2):
                         transpose_h(j + 2, i)
-                    else:
-                        transpose_fields(j + 2, i - TILES // 2)
-            if entry(j + 2):
-                write_last_rows(j + 2)
+                elif entry(j + 1):
+                    transpose_fields(j + 1, i - TILES // 2)
+            if entry(j + 1):
+                write_last_rows(j + 1)
             if entry(j - 2):
-                for i in range(OUT_TILES_ON_SCALAR, TILES):
-                    second_product(j - 2, i)
-                store(j - 2)
+                for i in range(tiles_on_scalar, TILES):
+                    second_product_and_store(j - 2, i, False)
             if entry(j):
                 quantise_enhanced(j)
-            if entry(j + 3):
-                total_fields(j + 3)
+            if entry(j + 2):
+                total_fields(j + 2)
+
+        for j in range(-2, 1):
+            step(j)
+        prepare_weight(out_w_rows, out_w_codes, out_w_scales)
+        for j in range(1, B + 2):
+            step(j)

@@ -75,6 +75,7 @@ def tile_fieldinteractionoperators_pa_t_kernel(
         nc.sync.dma_start(out=kernels[:], in_=corr_kernels.rearrange("h l j -> (h l j)").partition_broadcast(P))
         nc.sync.dma_start(out=edge_rows[0:B, :], in_=fields[:, 0:TILES, :].rearrange("b n c -> b (n c)"))
         nc.sync.dma_start(out=edge_rows[B : 2 * B, :], in_=fields[:, N - TILES : N, :].rearrange("b n c -> b (n c)"))
+        nc.sync.dma_start(out=out_b_rows[0:1, :], in_=out_b.rearrange("(o c) -> o c", o=1))
         b3_planes = const.tile([P, PLANES], BF16)
         nc.sync.dma_start(
             out=b3_planes[:].rearrange("q (u e) -> q u e", e=2), in_=b3.rearrange("(u q e) -> q u e", u=HALVES, e=2)
@@ -104,7 +105,6 @@ def tile_fieldinteractionoperators_pa_t_kernel(
             out=out_w_rows[:].rearrange("m (a k) -> m a k", a=TILES),
             in_=out_w.rearrange("(a m) k -> m a k", a=TILES),
         )
-        nc.sync.dma_start(out=out_b_rows[0:1, :], in_=out_b.rearrange("(o c) -> o c", o=1))
 
         def rows_to_words(rows, grouped, pair):
             words = rows[:].bitcast(F32)
@@ -126,11 +126,11 @@ def tile_fieldinteractionoperators_pa_t_kernel(
         def quantise(grouped, codes, scales):
             nc.vector.quantize_mx(out=codes[:].bitcast(FP8X4), scales=scales[:], in_=grouped[:])
 
-        def prepare_weight(rows, codes, scales):
+        def weight_to_words(rows):
             grouped = work.tile([P, PLANES * D], BF16, tag="weight_grouped", bufs=1, align_bytes=64)
             for pair in range(TILES // 2):
                 rows_to_words(rows, grouped, pair)
-            quantise(grouped, codes, scales)
+            return grouped
 
 
         norm = const.tile([P, LAGS * SUMS], F32)
@@ -233,7 +233,7 @@ def tile_fieldinteractionoperators_pa_t_kernel(
 
         w3_codes = const.tile([P, D], U32, align_bytes=64)
         w3_scales = const.tile([P, D], U8, align_bytes=64)
-        prepare_weight(w3_rows, w3_codes, w3_scales)
+        quantise(weight_to_words(w3_rows), w3_codes, w3_scales)
 
         out_bias_ps = products.tile([P, BANK], F32, tag="product")
         nc.tensor.matmul(out=out_bias_ps[:], lhsT=ones[:], rhs=out_b_rows[:], start=True, stop=True)
@@ -433,6 +433,8 @@ def tile_fieldinteractionoperators_pa_t_kernel(
 
         for j in range(-2, 1):
             step(j)
-        prepare_weight(out_w_rows, out_w_codes, out_w_scales)
-        for j in range(1, B + 2):
+        out_w_grouped = weight_to_words(out_w_rows)
+        step(1)
+        quantise(out_w_grouped, out_w_codes, out_w_scales)
+        for j in range(2, B + 2):
             step(j)

@@ -13,25 +13,44 @@ ACT = mybir.ActivationFunctionType
 AXIS = mybir.AxisListType
 
 P = 128
+QUADRANT = 32
+BANK = 512
 B = 16
 N = 512
 D = 512
 HEADS = 8
 LAGS = 3
+STREAMS = 2
 TILES = N // P
 PLANES = 4
-HALVES = 2
+WORD = 2
+HALVES = PLANES // WORD
+ROW_WORDS = D // WORD
 ROW = TILES * D
-BANK = 512
+BLOCKS_IN_BANK = BANK // (HALVES * P)
+
 KERNEL_CHANNELS = 4
+GROUPS = HEADS // HALVES
+PAIRS = KERNEL_CHANNELS // WORD
 SUMS = HEADS * KERNEL_CHANNELS
-CANDIDATES = 8
+CANDIDATES = GROUPS * PAIRS
 SLOTS = CANDIDATES + LAGS + 1
-SCALES = TILES * PLANES
+FIELD_SCALES = TILES * PLANES
 TERMS = (TILES - 1) * PLANES * SLOTS
+
 PRELOADED = 3
 LOADS_AHEAD = 4
+H_AHEAD = 2
+FIELDS_AHEAD = 1
+SECOND_PRODUCT_BEHIND = 2
+FIRST_STEP = -H_AHEAD
 OUT_TILES_ON_SCALAR = 2
+WORK_BUFFERS = 2
+RESULT_BUFFERS = 3
+BANKS_IN_RUN = 2
+WORD_BANKS = 3
+PRODUCT_BANKS = 4
+TOTAL_BANKS = 1
 
 FLOPS = 2 * 2 * B * N * D * D
 
@@ -44,11 +63,11 @@ def tile_fieldinteractionoperators_pa_t_kernel(
         ctx.enter_context(tc.manual_schedule())
         const = ctx.enter_context(tc.tile_pool(name="const", bufs=1))
         rows_in = ctx.enter_context(tc.tile_pool(name="rows_in", bufs=LOADS_AHEAD))
-        work = ctx.enter_context(tc.tile_pool(name="work", bufs=2))
-        rows_out = ctx.enter_context(tc.tile_pool(name="rows_out", bufs=3))
-        transposed = ctx.enter_context(tc.psum_pool(name="transposed", bufs=3))
-        products = ctx.enter_context(tc.psum_pool(name="products", bufs=4))
-        totals = ctx.enter_context(tc.psum_pool(name="totals", bufs=1))
+        work = ctx.enter_context(tc.tile_pool(name="work", bufs=WORK_BUFFERS))
+        rows_out = ctx.enter_context(tc.tile_pool(name="rows_out", bufs=RESULT_BUFFERS))
+        transposed = ctx.enter_context(tc.psum_pool(name="transposed", bufs=WORD_BANKS))
+        products = ctx.enter_context(tc.psum_pool(name="products", bufs=PRODUCT_BANKS))
+        totals = ctx.enter_context(tc.psum_pool(name="totals", bufs=TOTAL_BANKS))
 
         identity = const.tile([P, P], F32)
         make_identity(nc, identity[:])
@@ -58,18 +77,18 @@ def tile_fieldinteractionoperators_pa_t_kernel(
         zero_column = const.tile([P, 1], F32)
         nc.vector.memset(zero_column[:], 0.0)
         edge_rows = const.tile([P, ROW], BF16)
-        nc.vector.memset(edge_rows[32:64, :], 0.0)
-        nc.vector.memset(edge_rows[64:P, :], 0.0)
+        nc.vector.memset(edge_rows[QUADRANT : 2 * QUADRANT, :], 0.0)
+        nc.vector.memset(edge_rows[2 * QUADRANT : P, :], 0.0)
         out_b_rows = const.tile([P, D], BF16)
         nc.vector.memset(out_b_rows[:], 0.0)
         ones = const.tile([P, P], BF16)
         nc.vector.memset(ones[:], 1.0)
-        scales_all = const.tile([P, B * SCALES], F32)
+        scales_all = const.tile([P, B * FIELD_SCALES], F32)
         nc.vector.memset(scales_all[:], 1.0)
         weights = const.tile([P, (LAGS + 2) * SUMS], F32)
         nc.vector.memset(weights[:], 0.0)
 
-        logits = const.tile([P, 2], BF16)
+        logits = const.tile([P, STREAMS], BF16)
         nc.sync.dma_start(out=logits[:], in_=inter_w.partition_broadcast(P))
         kernels = const.tile([P, HEADS * LAGS * LAGS], BF16)
         nc.sync.dma_start(out=kernels[:], in_=corr_kernels.rearrange("h l j -> (h l j)").partition_broadcast(P))
@@ -78,13 +97,14 @@ def tile_fieldinteractionoperators_pa_t_kernel(
         nc.sync.dma_start(out=out_b_rows[0:1, :], in_=out_b.rearrange("(o c) -> o c", o=1))
         b3_planes = const.tile([P, PLANES], BF16)
         nc.sync.dma_start(
-            out=b3_planes[:].rearrange("q (u e) -> q u e", e=2), in_=b3.rearrange("(u q e) -> q u e", u=HALVES, e=2)
+            out=b3_planes[:].rearrange("q (u e) -> q u e", e=WORD),
+            in_=b3.rearrange("(u q e) -> q u e", u=HALVES, e=WORD),
         )
 
         w3_rows = const.tile([P, ROW], BF16)
         nc.sync.dma_start(
             out=w3_rows[:].rearrange("m (u x) -> m u x", u=HALVES),
-            in_=w3.rearrange("(u m e) k -> m u (e k)", u=HALVES, e=2),
+            in_=w3.rearrange("(u m e) k -> m u (e k)", u=HALVES, e=WORD),
         )
 
         h_rows = {}
@@ -110,17 +130,19 @@ def tile_fieldinteractionoperators_pa_t_kernel(
             words = rows[:].bitcast(F32)
             grouped_words = grouped[:].bitcast(F32)
             bank = transposed.tile([P, BANK], F32, tag="words")
-            for k in range(2):
+            for k in range(BLOCKS_IN_BANK):
                 for u in range(HALVES):
-                    first = (2 * pair + k) * (D // 2) + u * P
+                    first_word = (BLOCKS_IN_BANK * pair + k) * ROW_WORDS + u * P
                     nc.tensor.transpose(
                         bank[:, (HALVES * k + u) * P : (HALVES * k + u + 1) * P],
-                        words[:, first : first + P],
+                        words[:, first_word : first_word + P],
                         identity[:],
                     )
             nc.scalar.copy(
-                out=grouped_words[:, pair * BANK : (pair + 1) * BANK].rearrange("q (k r u) -> q k r u", k=2, u=HALVES),
-                in_=bank[:].rearrange("q (k u r) -> q k r u", k=2, u=HALVES),
+                out=grouped_words[:, pair * BANK : (pair + 1) * BANK].rearrange(
+                    "q (k r u) -> q k r u", k=BLOCKS_IN_BANK, u=HALVES
+                ),
+                in_=bank[:].rearrange("q (k u r) -> q k r u", k=BLOCKS_IN_BANK, u=HALVES),
             )
 
         def quantise(grouped, codes, scales):
@@ -128,20 +150,20 @@ def tile_fieldinteractionoperators_pa_t_kernel(
 
         def weight_to_words(rows):
             grouped = work.tile([P, PLANES * D], BF16, tag="weight_grouped", bufs=1, align_bytes=64)
-            for pair in range(TILES // 2):
+            for pair in range(TILES // BLOCKS_IN_BANK):
                 rows_to_words(rows, grouped, pair)
             return grouped
 
 
         norm = const.tile([P, LAGS * SUMS], F32)
-        lives_here = identity[:].rearrange("p (g x) -> p g x", x=32)[:, :, 0:2].unsqueeze(1)
+        lives_here = identity[:].rearrange("p (g x) -> p g x", x=QUADRANT)[:, :, 0:PAIRS].unsqueeze(1)
         for lag in range(1, LAGS + 1):
-            for e in range(2):
+            for e in range(WORD):
                 nc.vector.tensor_scalar_mul(
-                    out=norm[:].rearrange("p (l u g r e) -> p l u g r e", l=LAGS, u=HALVES, g=4, e=2)[
+                    out=norm[:].rearrange("p (l u g r e) -> p l u g r e", l=LAGS, u=HALVES, g=GROUPS, e=WORD)[
                         :, lag - 1, :, :, :, e
                     ],
-                    in0=lives_here.to_broadcast([P, HALVES, 4, 2]),
+                    in0=lives_here.to_broadcast([P, HALVES, GROUPS, PAIRS]),
                     scalar1=1.0 / (LAGS * (N - lag)),
                 )
 
@@ -159,45 +181,48 @@ def tile_fieldinteractionoperators_pa_t_kernel(
         nc.vector.tensor_tensor(out=top[:], in0=logits[:, 0:1], in1=logits[:, 1:2], op=ALU.max)
         minus_top = const.tile([P, 1], F32)
         nc.vector.tensor_scalar_mul(out=minus_top[:], in0=top[:], scalar1=-1.0)
-        exps = const.tile([P, 2], F32)
+        exps = const.tile([P, STREAMS], F32)
         exp_sum = const.tile([P, 1], F32)
         nc.scalar.activation(
             out=exps[:], in_=logits[:], func=ACT.Exp, bias=minus_top[:, 0:1], scale=1.0, accum_out=exp_sum[:, 0:1]
         )
-        for block in (1, 0):
+        for lag in range(2, LAGS + 1):
+            block = LAGS - lag
             nc.vector.tensor_tensor(
                 out=weights[:, block * SUMS : (block + 1) * SUMS],
                 in0=weights[:, (block + 1) * SUMS : (block + 2) * SUMS],
-                in1=weights[:, (4 - block) * SUMS : (5 - block) * SUMS],
+                in1=weights[:, (lag + 1) * SUMS : (lag + 2) * SUMS],
                 op=ALU.add,
             )
         plane_weight = const.tile([P, PLANES * LAGS], F32)
         for u in range(HALVES):
             nc.vector.tensor_reduce(
-                out=plane_weight[:, u * 2 * LAGS : (u + 1) * 2 * LAGS].rearrange("p (l e) -> p l e", e=2),
-                in_=own.rearrange("p (l u m e) -> p u l e m", l=LAGS, u=HALVES, e=2)[:, u],
+                out=plane_weight[:, u * WORD * LAGS : (u + 1) * WORD * LAGS].rearrange("p (l e) -> p l e", e=WORD),
+                in_=own.rearrange("p (l u m e) -> p u l e m", l=LAGS, u=HALVES, e=WORD)[:, u],
                 axis=AXIS.X,
                 op=ALU.add,
             )
 
         heads = const.tile([P, B * PLANES * LAGS], F32)
-        last_tokens = const.tile([P, B * SCALES], F32)
+        last_tokens = const.tile([P, B * FIELD_SCALES], F32)
         edge_words = edge_rows[:].bitcast(F32)
         for u in range(HALVES):
             edge_bank = transposed.tile([P, BANK], F32, tag="words")
             for n in range(TILES):
-                first = n * (D // 2) + u * P
-                nc.tensor.transpose(edge_bank[:, n * P : (n + 1) * P], edge_words[:, first : first + P], identity[:])
-            edge_values = edge_bank[:].bitcast(BF16).rearrange("q (n c e) -> q n c e", n=TILES, e=2)
+                first_word = n * ROW_WORDS + u * P
+                nc.tensor.transpose(
+                    edge_bank[:, n * P : (n + 1) * P], edge_words[:, first_word : first_word + P], identity[:]
+                )
+            edge_values = edge_bank[:].bitcast(BF16).rearrange("q (n c e) -> q n c e", n=TILES, e=WORD)
             nc.vector.tensor_copy(
-                out=heads[:].rearrange("q (b u n e) -> q n b u e", b=B, u=HALVES, e=2)[:, :, :, u, :],
+                out=heads[:].rearrange("q (b u n e) -> q n b u e", b=B, u=HALVES, e=WORD)[:, :, :, u, :],
                 in_=edge_values[:, 0:LAGS, 0:B, :],
             )
             nc.vector.tensor_copy(
-                out=last_tokens[:].rearrange("q (b n u e) -> q n b u e", b=B, n=TILES, e=2)[:, :, :, u, :],
+                out=last_tokens[:].rearrange("q (b n u e) -> q n b u e", b=B, n=TILES, e=WORD)[:, :, :, u, :],
                 in_=edge_values[:, :, B : 2 * B, :],
             )
-        heads_bune = heads[:].rearrange("q (b u n e) -> q b u n e", b=B, u=HALVES, e=2)
+        heads_bune = heads[:].rearrange("q (b u n e) -> q b u n e", b=B, u=HALVES, e=WORD)
         for n in range(1, LAGS):
             nc.vector.tensor_tensor(
                 out=heads_bune[:, :, :, n, :], in0=heads_bune[:, :, :, n, :], in1=heads_bune[:, :, :, n - 1, :], op=ALU.add
@@ -205,7 +230,7 @@ def tile_fieldinteractionoperators_pa_t_kernel(
 
         inv_sum = const.tile([P, 1], F32)
         nc.vector.reciprocal(out=inv_sum[:], in_=exp_sum[:])
-        iw = const.tile([P, 2], F32)
+        iw = const.tile([P, STREAMS], F32)
         nc.vector.tensor_scalar_mul(out=iw[:], in0=exps[:], scalar1=inv_sum[:, 0:1])
         minus_iw0 = const.tile([P, 1], F32)
         nc.vector.tensor_scalar_mul(out=minus_iw0[:], in0=iw[:, 0:1], scalar1=-1.0)
@@ -213,12 +238,12 @@ def tile_fieldinteractionoperators_pa_t_kernel(
         nc.vector.tensor_scalar_mul(out=total_weight[:], in0=weights[:, 0 : (TILES - 1) * SUMS], scalar1=iw[:, 0:1])
         head_weight = const.tile([P, PLANES * LAGS], F32)
         nc.vector.tensor_scalar_mul(out=head_weight[:], in0=plane_weight[:], scalar1=minus_iw0[:, 0:1])
-        nc.vector.memset(terms_all[:].rearrange("q (a m e) -> q a m e", m=SLOTS, e=2)[:, :, SLOTS - 1, :], 1.0)
+        nc.vector.memset(terms_all[:].rearrange("q (a m e) -> q a m e", m=SLOTS, e=WORD)[:, :, SLOTS - 1, :], 1.0)
         for i in range(TILES - 1):
-            counted = 2 * (LAGS - i)
+            counted = WORD * (LAGS - i)
             nc.vector.tensor_tensor(
                 out=terms_all[:].rearrange("q (b i u x) -> q b i u x", b=B, i=TILES - 1, u=HALVES)[
-                    :, :, i, :, 2 * CANDIDATES : 2 * CANDIDATES + counted
+                    :, :, i, :, WORD * CANDIDATES : WORD * CANDIDATES + counted
                 ],
                 in0=heads[:].rearrange("q (b u x) -> q b u x", b=B, u=HALVES)[:, :, :, 0:counted],
                 in1=head_weight[:]
@@ -269,30 +294,32 @@ def tile_fieldinteractionoperators_pa_t_kernel(
         def field_scales_products(b):
             nc.vector.tensor_tensor(
                 out=terms_all[:, b * TERMS : (b + 1) * TERMS].rearrange("q (i u x) -> q i u x", i=TILES - 1, u=HALVES)[
-                    :, :, :, 0 : 2 * CANDIDATES
+                    :, :, :, 0 : WORD * CANDIDATES
                 ],
                 in0=field_totals[b][:]
                 .rearrange("q (u x) -> q u x", u=HALVES)
                 .unsqueeze(1)
-                .to_broadcast([P, TILES - 1, HALVES, 2 * CANDIDATES]),
+                .to_broadcast([P, TILES - 1, HALVES, WORD * CANDIDATES]),
                 in1=total_weight[:].rearrange("q (i u x) -> q i u x", i=TILES - 1, u=HALVES),
                 op=ALU.mult,
             )
 
         def field_scales_sums(b):
             nc.vector.tensor_reduce(
-                out=scales_all[:, b * SCALES : b * SCALES + (TILES - 1) * PLANES].rearrange("q (a e) -> q a e", e=2),
-                in_=terms_all[:, b * TERMS : (b + 1) * TERMS].rearrange("q (a m e) -> q a e m", m=SLOTS, e=2),
+                out=scales_all[:, b * FIELD_SCALES : b * FIELD_SCALES + (TILES - 1) * PLANES].rearrange(
+                    "q (a e) -> q a e", e=WORD
+                ),
+                in_=terms_all[:, b * TERMS : (b + 1) * TERMS].rearrange("q (a m e) -> q a e m", m=SLOTS, e=WORD),
                 axis=AXIS.X,
                 op=ALU.add,
             )
 
         def scale_last_rows(b):
-            scaled = work.tile([P, SCALES], F32, tag="last_scaled")
+            scaled = work.tile([P, FIELD_SCALES], F32, tag="last_scaled")
             nc.gpsimd.tensor_tensor(
                 out=scaled[:],
-                in0=last_tokens[:, b * SCALES : (b + 1) * SCALES],
-                in1=scales_all[:, b * SCALES : (b + 1) * SCALES],
+                in0=last_tokens[:, b * FIELD_SCALES : (b + 1) * FIELD_SCALES],
+                in1=scales_all[:, b * FIELD_SCALES : (b + 1) * FIELD_SCALES],
                 op=ALU.mult,
             )
             last_scaled[b] = scaled
@@ -318,17 +345,17 @@ def tile_fieldinteractionoperators_pa_t_kernel(
             f_words = f_rows[b][:].bitcast(F32)
             bank = transposed.tile([P, BANK], F32, tag="words")
             for i in range(TILES):
-                first = i * (D // 2) + u * P
-                nc.tensor.transpose(bank[:, i * P : (i + 1) * P], f_words[:, first : first + P], identity[:])
-            values = bank[:].bitcast(BF16).rearrange("q (x e) -> q x e", e=2)
-            for e in range(2):
-                t = 2 * u + e
+                first_word = i * ROW_WORDS + u * P
+                nc.tensor.transpose(bank[:, i * P : (i + 1) * P], f_words[:, first_word : first_word + P], identity[:])
+            values = bank[:].bitcast(BF16).rearrange("q (x e) -> q x e", e=WORD)
+            for e in range(WORD):
+                t = WORD * u + e
                 nc.scalar.activation(
                     out=field_terms[b][:, t * N : (t + 1) * N],
                     in_=values[:, :, e],
                     func=ACT.Identity,
                     bias=nl_bias[:, t : t + 1],
-                    scale=scales_all[:, b * SCALES + t : b * SCALES + t + 1],
+                    scale=scales_all[:, b * FIELD_SCALES + t : b * FIELD_SCALES + t + 1],
                 )
 
         def quantise_h(b):
@@ -395,46 +422,51 @@ def tile_fieldinteractionoperators_pa_t_kernel(
             else:
                 nc.vector.tensor_tensor(out=results[b][:, columns], in0=projected[:], in1=out_bias[:], op=ALU.add)
             if i % 2 == 1:
-                pair = slice((i - 1) * D, (i + 1) * D)
-                nc.sync.dma_start(out=out[b].rearrange("(p i) o -> p (i o)", i=TILES)[:, pair], in_=results[b][:, pair])
+                half = slice((i - 1) * D, (i + 1) * D)
+                nc.sync.dma_start(out=out[b].rearrange("(p i) o -> p (i o)", i=TILES)[:, half], in_=results[b][:, half])
 
         def entry(b):
             return 0 <= b < B
 
+        def transpose_a_bank(j, k):
+            if k < TILES // BLOCKS_IN_BANK:
+                if entry(j + H_AHEAD):
+                    transpose_h(j + H_AHEAD, k)
+            elif entry(j + FIELDS_AHEAD):
+                transpose_fields(j + FIELDS_AHEAD, k - TILES // BLOCKS_IN_BANK)
+
         def step(j):
             if PRELOADED <= j + LOADS_AHEAD < B:
                 load(j + LOADS_AHEAD)
-            if entry(j + 1):
-                field_scales_products(j + 1)
-                quantise_h(j + 1)
-                field_scales_sums(j + 1)
-                scale_last_rows(j + 1)
+            if entry(j + FIELDS_AHEAD):
+                field_scales_products(j + FIELDS_AHEAD)
+                quantise_h(j + FIELDS_AHEAD)
+                field_scales_sums(j + FIELDS_AHEAD)
+                scale_last_rows(j + FIELDS_AHEAD)
             tiles_on_scalar = OUT_TILES_ON_SCALAR if entry(j) else 0
-            if entry(j - 2):
+            if entry(j - SECOND_PRODUCT_BEHIND):
                 for i in range(tiles_on_scalar):
-                    second_product_and_store(j - 2, i, True)
+                    second_product_and_store(j - SECOND_PRODUCT_BEHIND, i, True)
             for i in range(TILES):
                 if entry(j):
                     first_product_and_fusion(j, i)
-                if i < TILES // 2:
-                    if entry(j + 2):
-                        transpose_h(j + 2, i)
-                elif entry(j + 1):
-                    transpose_fields(j + 1, i - TILES // 2)
-            if entry(j + 1):
-                write_last_rows(j + 1)
-            if entry(j - 2):
+                if (i + 1) % BANKS_IN_RUN == 0:
+                    for k in range(i + 1 - BANKS_IN_RUN, i + 1):
+                        transpose_a_bank(j, k)
+            if entry(j + FIELDS_AHEAD):
+                write_last_rows(j + FIELDS_AHEAD)
+            if entry(j - SECOND_PRODUCT_BEHIND):
                 for i in range(tiles_on_scalar, TILES):
-                    second_product_and_store(j - 2, i, False)
+                    second_product_and_store(j - SECOND_PRODUCT_BEHIND, i, False)
             if entry(j):
                 quantise_enhanced(j)
-            if entry(j + 2):
-                total_fields(j + 2)
+            if entry(j + H_AHEAD):
+                total_fields(j + H_AHEAD)
 
-        for j in range(-2, 1):
+        for j in range(FIRST_STEP, SECOND_PRODUCT_BEHIND - 1):
             step(j)
         out_w_grouped = weight_to_words(out_w_rows)
-        step(1)
+        step(SECOND_PRODUCT_BEHIND - 1)
         quantise(out_w_grouped, out_w_codes, out_w_scales)
-        for j in range(2, B + 2):
+        for j in range(SECOND_PRODUCT_BEHIND, B + SECOND_PRODUCT_BEHIND):
             step(j)

from contextlib import ExitStack

import concourse.mybir as mybir
from concourse.masks import make_identity

F32 = mybir.dt.float32
BF16 = mybir.dt.bfloat16
U32 = mybir.dt.uint32
U8 = mybir.dt.uint8
FP8X4 = mybir.dt.float8_e4m3fn_x4
ALU = mybir.AluOpType
ACT = mybir.ActivationFunctionType
AXIS = mybir.AxisListType

P = 128
QUADRANT = 32
BANK = 512
B = 16
N = 512
D = 512
HEADS = 8
LAGS = 3
STREAMS = 2
TILES = N // P
PLANES = 4
WORD = 2
HALVES = PLANES // WORD
ROW_WORDS = D // WORD
ROW = TILES * D
BLOCKS_IN_BANK = BANK // (HALVES * P)

KERNEL_CHANNELS = 4
GROUPS = HEADS // HALVES
PAIRS = KERNEL_CHANNELS // WORD
SUMS = HEADS * KERNEL_CHANNELS
CANDIDATES = GROUPS * PAIRS
SLOTS = CANDIDATES + LAGS + 1
FIELD_SCALES = TILES * PLANES
TERMS = (TILES - 1) * PLANES * SLOTS

PRELOADED = 3
LOADS_AHEAD = 4
H_AHEAD = 2
FIELDS_AHEAD = 1
SECOND_PRODUCT_BEHIND = 2
FIRST_STEP = -H_AHEAD
OUT_TILES_ON_SCALAR = 2
WORK_BUFFERS = 2
RESULT_BUFFERS = 3
BANKS_IN_RUN = 2
WORD_BANKS = 3
PRODUCT_BANKS = 4
TOTAL_BANKS = 1

FLOPS = 2 * 2 * B * N * D * D


def tile_fieldinteractionoperators_pa_t_kernel(
    tc, fields, h2, corr_kernels, w3, b3, out_w, out_b, inter_w, out
):
    nc = tc.nc
    with ExitStack() as ctx:
        ctx.enter_context(tc.manual_schedule())
        const = ctx.enter_context(tc.tile_pool(name="const", bufs=1))
        rows_in = ctx.enter_context(tc.tile_pool(name="rows_in", bufs=LOADS_AHEAD))
        work = ctx.enter_context(tc.tile_pool(name="work", bufs=WORK_BUFFERS))
        rows_out = ctx.enter_context(tc.tile_pool(name="rows_out", bufs=RESULT_BUFFERS))
        transposed = ctx.enter_context(tc.psum_pool(name="transposed", bufs=WORD_BANKS))
        products = ctx.enter_context(tc.psum_pool(name="products", bufs=PRODUCT_BANKS))
        totals = ctx.enter_context(tc.psum_pool(name="totals", bufs=TOTAL_BANKS))

        identity = const.tile([P, P], F32)
        make_identity(nc, identity[:])
        terms_all = const.tile([P, B * TERMS], F32)
        nc.gpsimd.memset(terms_all[:], 0.0)

        zero_column = const.tile([P, 1], F32)
        nc.vector.memset(zero_column[:], 0.0)
        edge_rows = const.tile([P, ROW], BF16)
        nc.vector.memset(edge_rows[QUADRANT : 2 * QUADRANT, :], 0.0)
        nc.vector.memset(edge_rows[2 * QUADRANT : P, :], 0.0)
        out_b_rows = const.tile([P, D], BF16)
        nc.vector.memset(out_b_rows[:], 0.0)
        ones = const.tile([P, P], BF16)
        nc.vector.memset(ones[:], 1.0)
        scales_all = const.tile([P, B * FIELD_SCALES], F32)
        nc.vector.memset(scales_all[:], 1.0)
        weights = const.tile([P, (LAGS + 2) * SUMS], F32)
        nc.vector.memset(weights[:], 0.0)

        logits = const.tile([P, STREAMS], BF16)
        nc.sync.dma_start(out=logits[:], in_=inter_w.partition_broadcast(P))
        kernels = const.tile([P, HEADS * LAGS * LAGS], BF16)
        nc.sync.dma_start(out=kernels[:], in_=corr_kernels.rearrange("h l j -> (h l j)").partition_broadcast(P))
        nc.sync.dma_start(out=edge_rows[0:B, :], in_=fields[:, 0:TILES, :].rearrange("b n c -> b (n c)"))
        nc.sync.dma_start(out=edge_rows[B : 2 * B, :], in_=fields[:, N - TILES : N, :].rearrange("b n c -> b (n c)"))
        nc.sync.dma_start(out=out_b_rows[0:1, :], in_=out_b.rearrange("(o c) -> o c", o=1))
        b3_planes = const.tile([P, PLANES], BF16)
        nc.sync.dma_start(
            out=b3_planes[:].rearrange("q (u e) -> q u e", e=WORD),
            in_=b3.rearrange("(u q e) -> q u e", u=HALVES, e=WORD),
        )

        w3_rows = const.tile([P, ROW], BF16)
        nc.sync.dma_start(
            out=w3_rows[:].rearrange("m (u x) -> m u x", u=HALVES),
            in_=w3.rearrange("(u m e) k -> m u (e k)", u=HALVES, e=WORD),
        )

        h_rows = {}
        f_rows = {}

        def load(b):
            h_tile = rows_in.tile([P, ROW], BF16, tag="h_rows")
            nc.sync.dma_start(out=h_tile[:], in_=h2[b].rearrange("(p i) c -> p (i c)", i=TILES))
            h_rows[b] = h_tile
            f_tile = rows_in.tile([P, ROW], BF16, tag="f_rows")
            nc.sync.dma_start(out=f_tile[:], in_=fields[b].rearrange("(p i) c -> p (i c)", i=TILES))
            f_rows[b] = f_tile

        for b in range(PRELOADED):
            load(b)
        out_w_rows = const.tile([P, ROW], BF16)
        nc.sync.dma_start(
            out=out_w_rows[:].rearrange("m (a k) -> m a k", a=TILES),
            in_=out_w.rearrange("(a m) k -> m a k", a=TILES),
        )

        def rows_to_words(rows, grouped, pair):
            words = rows[:].bitcast(F32)
            grouped_words = grouped[:].bitcast(F32)
            bank = transposed.tile([P, BANK], F32, tag="words")
            for k in range(BLOCKS_IN_BANK):
                for u in range(HALVES):
                    first_word = (BLOCKS_IN_BANK * pair + k) * ROW_WORDS + u * P
                    nc.tensor.transpose(
                        bank[:, (HALVES * k + u) * P : (HALVES * k + u + 1) * P],
                        words[:, first_word : first_word + P],
                        identity[:],
                    )
            nc.scalar.copy(
                out=grouped_words[:, pair * BANK : (pair + 1) * BANK].rearrange(
                    "q (k r u) -> q k r u", k=BLOCKS_IN_BANK, u=HALVES
                ),
                in_=bank[:].rearrange("q (k u r) -> q k r u", k=BLOCKS_IN_BANK, u=HALVES),
            )

        def quantise(grouped, codes, scales):
            nc.vector.quantize_mx(out=codes[:].bitcast(FP8X4), scales=scales[:], in_=grouped[:])

        def weight_to_words(rows):
            grouped = work.tile([P, PLANES * D], BF16, tag="weight_grouped", bufs=1, align_bytes=64)
            for pair in range(TILES // BLOCKS_IN_BANK):
                rows_to_words(rows, grouped, pair)
            return grouped


        norm = const.tile([P, LAGS * SUMS], F32)
        lives_here = identity[:].rearrange("p (g x) -> p g x", x=QUADRANT)[:, :, 0:PAIRS].unsqueeze(1)
        for lag in range(1, LAGS + 1):
            for e in range(WORD):
                nc.vector.tensor_scalar_mul(
                    out=norm[:].rearrange("p (l u g r e) -> p l u g r e", l=LAGS, u=HALVES, g=GROUPS, e=WORD)[
                        :, lag - 1, :, :, :, e
                    ],
                    in0=lives_here.to_broadcast([P, HALVES, GROUPS, PAIRS]),
                    scalar1=1.0 / (LAGS * (N - lag)),
                )

        warm = const.tile([P, 1], F32)
        nc.scalar.activation(out=warm[:], in_=zero_column[:], func=ACT.Exp)

        own = weights[:, 2 * SUMS :]
        nc.vector.tensor_tensor(
            out=own.rearrange("p (l h j) -> p l h j", l=LAGS, h=HEADS)[:, :, :, 0:LAGS],
            in0=kernels[:].rearrange("p (h l j) -> p l h j", h=HEADS, l=LAGS),
            in1=norm[:].rearrange("p (l h j) -> p l h j", l=LAGS, h=HEADS)[:, :, :, 0:LAGS],
            op=ALU.mult,
        )
        top = const.tile([P, 1], F32)
        nc.vector.tensor_tensor(out=top[:], in0=logits[:, 0:1], in1=logits[:, 1:2], op=ALU.max)
        minus_top = const.tile([P, 1], F32)
        nc.vector.tensor_scalar_mul(out=minus_top[:], in0=top[:], scalar1=-1.0)
        exps = const.tile([P, STREAMS], F32)
        exp_sum = const.tile([P, 1], F32)
        nc.scalar.activation(
            out=exps[:], in_=logits[:], func=ACT.Exp, bias=minus_top[:, 0:1], scale=1.0, accum_out=exp_sum[:, 0:1]
        )
        for lag in range(2, LAGS + 1):
            block = LAGS - lag
            nc.vector.tensor_tensor(
                out=weights[:, block * SUMS : (block + 1) * SUMS],
                in0=weights[:, (block + 1) * SUMS : (block + 2) * SUMS],
                in1=weights[:, (lag + 1) * SUMS : (lag + 2) * SUMS],
                op=ALU.add,
            )
        plane_weight = const.tile([P, PLANES * LAGS], F32)
        for u in range(HALVES):
            nc.vector.tensor_reduce(
                out=plane_weight[:, u * WORD * LAGS : (u + 1) * WORD * LAGS].rearrange("p (l e) -> p l e", e=WORD),
                in_=own.rearrange("p (l u m e) -> p u l e m", l=LAGS, u=HALVES, e=WORD)[:, u],
                axis=AXIS.X,
                op=ALU.add,
            )

        heads = const.tile([P, B * PLANES * LAGS], F32)
        last_tokens = const.tile([P, B * FIELD_SCALES], F32)
        edge_words = edge_rows[:].bitcast(F32)
        for u in range(HALVES):
            edge_bank = transposed.tile([P, BANK], F32, tag="words")
            for n in range(TILES):
                first_word = n * ROW_WORDS + u * P
                nc.tensor.transpose(
                    edge_bank[:, n * P : (n + 1) * P], edge_words[:, first_word : first_word + P], identity[:]
                )
            edge_values = edge_bank[:].bitcast(BF16).rearrange("q (n c e) -> q n c e", n=TILES, e=WORD)
            nc.vector.tensor_copy(
                out=heads[:].rearrange("q (b u n e) -> q n b u e", b=B, u=HALVES, e=WORD)[:, :, :, u, :],
                in_=edge_values[:, 0:LAGS, 0:B, :],
            )
            nc.vector.tensor_copy(
                out=last_tokens[:].rearrange("q (b n u e) -> q n b u e", b=B, n=TILES, e=WORD)[:, :, :, u, :],
                in_=edge_values[:, :, B : 2 * B, :],
            )
        heads_bune = heads[:].rearrange("q (b u n e) -> q b u n e", b=B, u=HALVES, e=WORD)
        for n in range(1, LAGS):
            nc.vector.tensor_tensor(
                out=heads_bune[:, :, :, n, :], in0=heads_bune[:, :, :, n, :], in1=heads_bune[:, :, :, n - 1, :], op=ALU.add
            )

        inv_sum = const.tile([P, 1], F32)
        nc.vector.reciprocal(out=inv_sum[:], in_=exp_sum[:])
        iw = const.tile([P, STREAMS], F32)
        nc.vector.tensor_scalar_mul(out=iw[:], in0=exps[:], scalar1=inv_sum[:, 0:1])
        minus_iw0 = const.tile([P, 1], F32)
        nc.vector.tensor_scalar_mul(out=minus_iw0[:], in0=iw[:, 0:1], scalar1=-1.0)
        total_weight = const.tile([P, (TILES - 1) * SUMS], F32)
        nc.vector.tensor_scalar_mul(out=total_weight[:], in0=weights[:, 0 : (TILES - 1) * SUMS], scalar1=iw[:, 0:1])
        head_weight = const.tile([P, PLANES * LAGS], F32)
        nc.vector.tensor_scalar_mul(out=head_weight[:], in0=plane_weight[:], scalar1=minus_iw0[:, 0:1])
        nc.vector.memset(terms_all[:].rearrange("q (a m e) -> q a m e", m=SLOTS, e=WORD)[:, :, SLOTS - 1, :], 1.0)
        for i in range(TILES - 1):
            counted = WORD * (LAGS - i)
            nc.vector.tensor_tensor(
                out=terms_all[:].rearrange("q (b i u x) -> q b i u x", b=B, i=TILES - 1, u=HALVES)[
                    :, :, i, :, WORD * CANDIDATES : WORD * CANDIDATES + counted
                ],
                in0=heads[:].rearrange("q (b u x) -> q b u x", b=B, u=HALVES)[:, :, :, 0:counted],
                in1=head_weight[:]
                .rearrange("q (u x) -> q u x", u=HALVES)[:, :, 0:counted]
                .unsqueeze(1)
                .to_broadcast([P, B, HALVES, counted]),
                op=ALU.mult,
            )

        nl_bias = const.tile([P, PLANES], F32)
        nc.vector.tensor_scalar_mul(out=nl_bias[:], in0=b3_planes[:], scalar1=iw[:, 1:2])

        w3_codes = const.tile([P, D], U32, align_bytes=64)
        w3_scales = const.tile([P, D], U8, align_bytes=64)
        quantise(weight_to_words(w3_rows), w3_codes, w3_scales)

        out_bias_ps = products.tile([P, BANK], F32, tag="product")
        nc.tensor.matmul(out=out_bias_ps[:], lhsT=ones[:], rhs=out_b_rows[:], start=True, stop=True)
        out_bias = const.tile([P, D], F32)
        nc.vector.tensor_copy(out=out_bias[:], in_=out_bias_ps[:])

        h_grouped = {}
        h_codes = {}
        h_scales = {}
        field_totals = {}
        field_terms = {}
        last_scaled = {}
        enhanced = {}
        e_codes = {}
        e_scales = {}
        results = {}
        out_w_codes = const.tile([P, D], U32, align_bytes=64)
        out_w_scales = const.tile([P, D], U8, align_bytes=64)

        def total_fields(b):
            total = totals.tile([P, SUMS], F32, tag="total")
            kernel_channels = f_rows[b][:].rearrange("p (i h x) -> p i h x", i=TILES, h=HEADS)
            for i in range(TILES):
                nc.tensor.matmul(
                    out=total[:].rearrange("p (h j) -> p h j", h=HEADS),
                    lhsT=ones[:],
                    rhs=kernel_channels[:, i, :, 0:KERNEL_CHANNELS],
                    start=(i == 0),
                    stop=(i == TILES - 1),
                )
            field_totals[b] = total

        def field_scales_products(b):
            nc.vector.tensor_tensor(
                out=terms_all[:, b * TERMS : (b + 1) * TERMS].rearrange("q (i u x) -> q i u x", i=TILES - 1, u=HALVES)[
                    :, :, :, 0 : WORD * CANDIDATES
                ],
                in0=field_totals[b][:]
                .rearrange("q (u x) -> q u x", u=HALVES)
                .unsqueeze(1)
                .to_broadcast([P, TILES - 1, HALVES, WORD * CANDIDATES]),
                in1=total_weight[:].rearrange("q (i u x) -> q i u x", i=TILES - 1, u=HALVES),
                op=ALU.mult,
            )

        def field_scales_sums(b):
            nc.vector.tensor_reduce(
                out=scales_all[:, b * FIELD_SCALES : b * FIELD_SCALES + (TILES - 1) * PLANES].rearrange(
                    "q (a e) -> q a e", e=WORD
                ),
                in_=terms_all[:, b * TERMS : (b + 1) * TERMS].rearrange("q (a m e) -> q a e m", m=SLOTS, e=WORD),
                axis=AXIS.X,
                op=ALU.add,
            )

        def scale_last_rows(b):
            scaled = work.tile([P, FIELD_SCALES], F32, tag="last_scaled")
            nc.gpsimd.tensor_tensor(
                out=scaled[:],
                in0=last_tokens[:, b * FIELD_SCALES : (b + 1) * FIELD_SCALES],
                in1=scales_all[:, b * FIELD_SCALES : (b + 1) * FIELD_SCALES],
                op=ALU.mult,
            )
            last_scaled[b] = scaled

        def write_last_rows(b):
            nc.gpsimd.tensor_tensor(
                out=field_terms[b][:].rearrange("q (t i r) -> q i t r", t=PLANES, i=TILES)[:, :, :, P - 1],
                in0=last_scaled[b][:].rearrange("q (i t) -> q i t", i=TILES),
                in1=nl_bias[:].unsqueeze(1).to_broadcast([P, TILES, PLANES]),
                op=ALU.add,
            )

        def transpose_h(b, pair):
            if pair == 0:
                grouped = work.tile([P, PLANES * N], BF16, tag="h_grouped", align_bytes=64)
                h_grouped[b] = grouped
            rows_to_words(h_rows[b], h_grouped[b], pair)

        def transpose_fields(b, u):
            if u == 0:
                term = work.tile([P, PLANES * N], F32, tag="field_term")
                field_terms[b] = term
            f_words = f_rows[b][:].bitcast(F32)
            bank = transposed.tile([P, BANK], F32, tag="words")
            for i in range(TILES):
                first_word = i * ROW_WORDS + u * P
                nc.tensor.transpose(bank[:, i * P : (i + 1) * P], f_words[:, first_word : first_word + P], identity[:])
            values = bank[:].bitcast(BF16).rearrange("q (x e) -> q x e", e=WORD)
            for e in range(WORD):
                t = WORD * u + e
                nc.scalar.activation(
                    out=field_terms[b][:, t * N : (t + 1) * N],
                    in_=values[:, :, e],
                    func=ACT.Identity,
                    bias=nl_bias[:, t : t + 1],
                    scale=scales_all[:, b * FIELD_SCALES + t : b * FIELD_SCALES + t + 1],
                )

        def quantise_h(b):
            codes = work.tile([P, N], U32, tag="h_codes", align_bytes=64)
            scales = work.tile([P, N], U8, tag="h_scales", align_bytes=64)
            quantise(h_grouped[b], codes, scales)
            h_codes[b] = codes
            h_scales[b] = scales

        def first_product_and_fusion(b, i):
            if i == 0:
                fused = work.tile([P, PLANES * N], BF16, tag="enhanced", align_bytes=64)
                enhanced[b] = fused
            tokens = slice(i * P, (i + 1) * P)
            nl = products.tile([P, BANK], F32, tag="product")
            for t in range(PLANES):
                channels = slice(t * P, (t + 1) * P)
                nc.tensor.matmul_mx(
                    out=nl[:, channels],
                    lhsT=w3_codes[:, channels].bitcast(FP8X4),
                    lhsT_scale=w3_scales[:, channels],
                    rhs=h_codes[b][:, tokens].bitcast(FP8X4),
                    rhs_scale=h_scales[b][:, tokens],
                    start=True,
                    stop=True,
                )
            nc.vector.scalar_tensor_tensor(
                out=enhanced[b][:, i * BANK : (i + 1) * BANK].rearrange("q (r t) -> q r t", t=PLANES),
                in0=nl[:].rearrange("q (t r) -> q r t", t=PLANES),
                scalar=iw[:, 1:2],
                in1=field_terms[b][:].rearrange("q (t i r) -> q i r t", t=PLANES, i=TILES)[:, i],
                op0=ALU.mult,
                op1=ALU.add,
            )

        def quantise_enhanced(b):
            codes = work.tile([P, N], U32, tag="e_codes", align_bytes=64)
            scales = work.tile([P, N], U8, tag="e_scales", align_bytes=64)
            quantise(enhanced[b], codes, scales)
            e_codes[b] = codes
            e_scales[b] = scales

        def second_product_and_store(b, i, on_scalar):
            if i == 0:
                result = rows_out.tile([P, TILES * D], F32, tag="result")
                results[b] = result
            tokens = slice(i * P, (i + 1) * P)
            columns = slice(i * D, (i + 1) * D)
            projected = products.tile([P, BANK], F32, tag="product")
            nc.tensor.matmul_mx(
                out=projected[:],
                lhsT=e_codes[b][:, tokens].bitcast(FP8X4),
                lhsT_scale=e_scales[b][:, tokens],
                rhs=out_w_codes[:].bitcast(FP8X4),
                rhs_scale=out_w_scales[:],
                start=True,
                stop=True,
            )
            if on_scalar:
                nc.scalar.copy(out=results[b][:, columns], in_=projected[:])
                nc.gpsimd.tensor_tensor(
                    out=results[b][:, columns], in0=results[b][:, columns], in1=out_bias[:], op=ALU.add
                )
            else:
                nc.vector.tensor_tensor(out=results[b][:, columns], in0=projected[:], in1=out_bias[:], op=ALU.add)
            if i % 2 == 1:
                half = slice((i - 1) * D, (i + 1) * D)
                nc.sync.dma_start(out=out[b].rearrange("(p i) o -> p (i o)", i=TILES)[:, half], in_=results[b][:, half])

        def entry(b):
            return 0 <= b < B

        def transpose_a_bank(j, k):
            if k < TILES // BLOCKS_IN_BANK:
                if entry(j + H_AHEAD):
                    transpose_h(j + H_AHEAD, k)
            elif entry(j + FIELDS_AHEAD):
                transpose_fields(j + FIELDS_AHEAD, k - TILES // BLOCKS_IN_BANK)

        def step(j):
            if PRELOADED <= j + LOADS_AHEAD < B:
                load(j + LOADS_AHEAD)
            if entry(j + FIELDS_AHEAD):
                field_scales_products(j + FIELDS_AHEAD)
                quantise_h(j + FIELDS_AHEAD)
                field_scales_sums(j + FIELDS_AHEAD)
                scale_last_rows(j + FIELDS_AHEAD)
            tiles_on_scalar = OUT_TILES_ON_SCALAR if entry(j) else 0
            if entry(j - SECOND_PRODUCT_BEHIND):
                for i in range(tiles_on_scalar):
                    second_product_and_store(j - SECOND_PRODUCT_BEHIND, i, True)
            for i in range(TILES):
                if entry(j):
                    first_product_and_fusion(j, i)
                if (i + 1) % BANKS_IN_RUN == 0:
                    for k in range(i + 1 - BANKS_IN_RUN, i + 1):
                        transpose_a_bank(j, k)
            if entry(j + FIELDS_AHEAD):
                write_last_rows(j + FIELDS_AHEAD)
            if entry(j - SECOND_PRODUCT_BEHIND):
                for i in range(tiles_on_scalar, TILES):
                    second_product_and_store(j - SECOND_PRODUCT_BEHIND, i, False)
            if entry(j):
                quantise_enhanced(j)
            if entry(j + H_AHEAD):
                total_fields(j + H_AHEAD)

        for j in range(FIRST_STEP, SECOND_PRODUCT_BEHIND - 1):
            step(j)
        out_w_grouped = weight_to_words(out_w_rows)
        step(SECOND_PRODUCT_BEHIND - 1)
        quantise(out_w_grouped, out_w_codes, out_w_scales)
        for j in range(SECOND_PRODUCT_BEHIND, B + SECOND_PRODUCT_BEHIND):
            step(j)
